import numpy as np
import ml_dtypes


def mxq(x, axis, fmt="e4m3"):
    dtype, down = {"e4m3": (ml_dtypes.float8_e4m3fn, 7), "e5m2": (ml_dtypes.float8_e5m2, 14)}[fmt]
    v = np.moveaxis(np.asarray(x, np.float32).astype(ml_dtypes.bfloat16).astype(np.float64), axis, -1)
    blocks = v.reshape(v.shape[:-1] + (-1, 32))
    amax = np.abs(blocks).max(-1, keepdims=True)
    byte = np.maximum(np.where(amax > 0, np.frexp(amax)[1] - 1 + 127, 0) - down, 1)
    scale = np.exp2(byte - 127.0)
    codes = (blocks / scale).astype(np.float32).astype(dtype).astype(np.float64)
    return np.moveaxis((codes * scale).reshape(v.shape), -1, axis)


WIDE = False


def mx_kscale(k):
    if not WIDE:
        return np.ones(k)
    levels = np.array([30, -30])
    if k % 512:
        return np.exp2(np.random.permutation(np.resize(levels, k // 32))).repeat(32)
    a = np.empty((k // 512, 16))
    for p in range(k // 512):
        a[p, :8] = np.random.permutation(np.resize(levels, 8))
        for g in range(8):
            far = levels[np.abs(levels - a[p, g]) >= 10]
            a[p, g + 8] = far[np.random.randint(len(far))]
    return np.exp2(a.ravel()).repeat(32)


BF16 = ml_dtypes.bfloat16


def bf(x):
    return np.asarray(x, np.float32).astype(BF16)


def f64(x):
    return np.asarray(x).astype(np.float64)


B, S, D, E = 4, 512, 1024, 1024
THETA = 10000.0


def rope_tables():
    inv = 1.0 / THETA ** (np.arange(0, E, 2).astype(np.float64) / E)
    ang = np.outer(np.arange(S).astype(np.float64), inv)
    return np.cos(ang), np.sin(ang)


def rotate(u, cos, sin):
    ur, ui = u[..., 0::2], u[..., 1::2]
    return np.stack([ur * cos - ui * sin, ur * sin + ui * cos], axis=-1).reshape(B, S, E)


def setup_inputs():
    s = mx_kscale(D)
    return {"x": bf(np.random.standard_normal((B, S, D)) * s),
            "wq": bf(np.random.standard_normal((E, D)) / np.sqrt(D) / s),
            "wk": bf(np.random.standard_normal((E, D)) / np.sqrt(D) / s)}


def reference(x, wq, wk):
    xm = mxq(f64(x), 2, "e5m2")
    xq = xm @ mxq(f64(wq), 1, "e4m3").T
    xk = xm @ mxq(f64(wk), 1, "e4m3").T
    cos, sin = rope_tables()
    return rotate(xq, cos, sin), rotate(xk, cos, sin)

@@ -1,0 +1,240 @@
+import math
+from contextlib import ExitStack
+
+import concourse.mybir as mybir
+from concourse.masks import make_identity
+
+B, S, D, E = 4, 512, 1024, 1024
+THETA = 10000.0
+FLOPS = 2 * 2 * B * S * D * E
+
+F32 = mybir.dt.float32
+BF16 = mybir.dt.bfloat16
+I32 = mybir.dt.int32
+U32 = mybir.dt.uint32
+U8 = mybir.dt.uint8
+E5M2X4 = mybir.dt.float8_e5m2_x4
+E4M3X4 = mybir.dt.float8_e4m3fn_x4
+ALU = mybir.AluOpType
+ACT = mybir.ActivationFunctionType
+
+P = 128
+PASSES = 2
+WORDS = 256
+COLS = 512
+PAIRS = 256
+GROUPS = S // P
+HALVES = E // COLS
+STEPS_PER_GROUP = 4
+STEPS = HALVES * GROUPS * STEPS_PER_GROUP
+
+
+def tile_attention_pa_kernel(tc, x, wq, wk, out_0, out_1):
+    nc = tc.nc
+    weights = (wq, wk)
+    outs = (out_0, out_1)
+
+    with ExitStack() as ctx:
+        keep = ctx.enter_context(tc.tile_pool(name="keep", bufs=1))
+        stage = ctx.enter_context(tc.tile_pool(name="stage", bufs=3))
+        work = ctx.enter_context(tc.tile_pool(name="work", bufs=3))
+        res = ctx.enter_context(tc.tile_pool(name="res", bufs=8))
+        tpsum = ctx.enter_context(tc.psum_pool(name="tpsum", bufs=3))
+        mpsum = ctx.enter_context(tc.psum_pool(name="mpsum", bufs=5))
+        ctx.enter_context(tc.manual_schedule())
+
+        x_raw = {}
+        w_raw = {}
+
+        def load_x_tile(j, b):
+            t = keep.tile([P, D], BF16, name=f"x_raw_{j}_{b}")
+            nc.sync.dma_start(out=t[:], in_=x[b, j * P:(j + 1) * P, :])
+            x_raw[(j, b)] = t[:]
+
+        def load_x_group(j):
+            t = keep.tile([P, B, D], BF16, name=f"x_raw_{j}")
+            nc.sync.dma_start(out=t[:], in_=x[:, j * P:(j + 1) * P, :].rearrange("b p k -> p b k"))
+            for b in range(B):
+                x_raw[(j, b)] = t[:, b, :]
+
+        def load_w_block(w, blk):
+            t = keep.tile([P, 2, D], BF16, name=f"w_raw_{w}_{blk}")
+            rows = weights[w][blk * 2 * P:(blk + 1) * 2 * P, :]
+            nc.sync.dma_start(out=t[:], in_=rows.rearrange("(m two) k -> m two k", two=2))
+            for two in range(2):
+                w_raw[(w, blk // 2, (blk % 2) * 2 + two)] = t[:, two, :]
+
+        load_x_tile(0, 0)
+        load_w_block(0, 0)
+        load_w_block(0, 1)
+        for b in range(1, B):
+            load_x_tile(0, b)
+        load_w_block(1, 0)
+        load_w_block(1, 1)
+        load_x_group(1)
+        load_x_group(2)
+        load_w_block(0, 2)
+        load_w_block(0, 3)
+        load_x_group(3)
+        load_w_block(1, 2)
+        load_w_block(1, 3)
+
+        ident = keep.tile([P, P], F32)
+        make_identity(nc, ident[:])
+        pos = keep.tile([P, GROUPS], F32)
+        nc.gpsimd.iota(pos[:], pattern=[[P, GROUPS]], base=0, channel_multiplier=1,
+                       allow_small_or_imprecise_dtypes=True)
+
+        one = keep.tile([P, 1], F32)
+        nc.vector.memset(one[:], 1.0)
+        freq = keep.tile([P, E // 2], F32)
+        half_pi = keep.tile([P, 1], F32)
+        nc.vector.tensor_scalar(out=freq[:, 0:1], in0=one[:], scalar1=1.0 / (2.0 * math.pi), scalar2=None, op0=ALU.mult)
+        nc.vector.tensor_scalar(out=half_pi[:], in0=one[:], scalar1=math.pi / 2.0, scalar2=None, op0=ALU.mult)
+        n = 1
+        while n < E // 2:
+            nc.vector.tensor_scalar(out=freq[:, n:2 * n], in0=freq[:, 0:n], scalar1=THETA ** (-2.0 * n / E),
+                                    scalar2=None, op0=ALU.mult)
+            n *= 2
+
+        whole = keep.tile([P, GROUPS, E // 2], I32)
+        frac = keep.tile([P, GROUPS, E // 2], F32)
+
+        def whole_turns(j):
+            nc.vector.tensor_scalar(out=whole[:, j, :], in0=freq[:], scalar1=pos[:, j:j + 1], scalar2=None, op0=ALU.mult)
+
+        def fraction(j):
+            nc.vector.scalar_tensor_tensor(out=frac[:, j, :], in0=freq[:], scalar=pos[:, j:j + 1], in1=whole[:, j, :],
+                                           op0=ALU.mult, op1=ALU.subtract)
+
+        whole_turns(0)
+        for j in range(GROUPS):
+            if j + 1 < GROUPS:
+                whole_turns(j + 1)
+            fraction(j)
+
+        tables = {}
+
+        def make_table(h, j):
+            t = keep.tile([P, 3, PAIRS], F32, name=f"table_{h}_{j}")
+            f = frac[:, j, h * PAIRS:(h + 1) * PAIRS]
+            mag = work.tile([P, PAIRS], F32, name="mag")
+            nc.scalar.activation(out=mag[:], in_=f, func=ACT.Abs)
+            nc.scalar.activation(out=t[:, 0, :], in_=f, func=ACT.Sin, scale=-2.0 * math.pi)
+            nc.scalar.activation(out=t[:, 2, :], in_=f, func=ACT.Sin, scale=2.0 * math.pi)
+            nc.scalar.activation(out=t[:, 1, :], in_=mag[:], func=ACT.Sin, scale=-2.0 * math.pi, bias=half_pi[:])
+            tables[(h, j)] = t
+
+        staged = {}
+        codes = {}
+        scales = {}
+
+        def transpose_rows(key, slot):
+            raw = x_raw[(key[1], slot)] if key[0] == "x" else w_raw[(key[1], key[2], slot)]
+            if slot == 0:
+                staged[key] = stage.tile([P, PASSES, COLS, 4], BF16, name="staged", align_bytes=256)
+                name = "_".join(str(v) for v in key)
+                codes[key] = keep.tile([P, PASSES, COLS], U32, name="codes_" + name, align_bytes=256)
+                scales[key] = keep.tile([P, PASSES, COLS], U8, name="scales_" + name, align_bytes=256)
+            words = raw.bitcast(F32)
+            bank = tpsum.tile([P, PASSES, 2, P], F32, name="tbank")
+            for g in range(PASSES):
+                for u in range(2):
+                    nc.tensor.transpose(bank[:, g, u, :], words[:, g * WORDS + u:(g + 1) * WORDS:2], ident[:])
+            dst = staged[key][:].rearrange("p g c t -> p g (c t)").bitcast(F32).rearrange("p g (c u) -> p g c u", u=2)
+            nc.scalar.copy(out=dst[:, :, slot * P:(slot + 1) * P, :], in_=bank[:].rearrange("p g u r -> p g r u"))
+
+        def quantize(key, first, count):
+            fmt = E5M2X4 if key[0] == "x" else E4M3X4
+            if count == 4:
+                nc.vector.quantize_mx(out=codes[key][:].rearrange("p g c -> p (g c)").bitcast(fmt),
+                                      scales=scales[key][:].rearrange("p g c -> p (g c)"),
+                                      in_=staged[key][:].rearrange("p g c t -> p (g c t)"))
+                return
+            cols = slice(first * P, (first + count) * P)
+            for g in range(PASSES):
+                nc.vector.quantize_mx(out=codes[key][:, g, cols].bitcast(fmt), scales=scales[key][:, g, cols],
+                                      in_=staged[key][:, g, cols, :].rearrange("p c t -> p (c t)"))
+
+        def step_indices(s):
+            h, j = s // (GROUPS * STEPS_PER_GROUP), (s // STEPS_PER_GROUP) % GROUPS
+            w, b0 = (s % STEPS_PER_GROUP) // 2, 2 * (s % 2)
+            return h, j, w, b0
+
+        banks = {}
+
+        def multiply(s):
+            h, j, w, b0 = step_indices(s)
+            xk, wkey = ("x", j), ("w", w, h)
+            for i in range(2):
+                bank = mpsum.tile([P, COLS], F32, name="mbank")
+                cols = slice((b0 + i) * P, (b0 + i + 1) * P)
+                for g in range(PASSES):
+                    nc.tensor.matmul_mx(out=bank[:], lhsT=codes[xk][:, g, cols].bitcast(E5M2X4),
+                                        lhsT_scale=scales[xk][:, g, cols],
+                                        rhs=codes[wkey][:, g, :].bitcast(E4M3X4), rhs_scale=scales[wkey][:, g, :],
+                                        start=(g == 0), stop=(g == PASSES - 1))
+                banks[(s, i)] = bank
+
+        def rotate(s):
+            h, j, w, b0 = step_indices(s)
+            table = tables[(h, j)]
+            from_even = work.tile([P, 2, COLS], F32, name="from_even")
+            from_odd = work.tile([P, 2, COLS], F32, name="from_odd")
+            last = s == STEPS - 1
+            dst = outs[w][b0:b0 + 2, j * P:(j + 1) * P, h * COLS:(h + 1) * COLS]
+            for i in range(2):
+                u = banks[(s, i)][:].rearrange("p (b two m) -> p b two m", two=2, m=P)
+                for two, part, lo in ((0, from_even, 1), (1, from_odd, 0)):
+                    nc.vector.tensor_tensor(
+                        out=part[:, i, :].rearrange("p (b m c) -> p b m c", m=P, c=2),
+                        in0=u[:, :, two, :].unsqueeze(3).to_broadcast([P, 2, P, 2]),
+                        in1=table[:, lo:lo + 2, :].rearrange("p c (b m) -> p b m c", m=P),
+                        op=ALU.mult)
+                if last:
+                    half = res.tile([P, COLS], F32, name="half", bufs=2)
+                    eng = nc.gpsimd if i == 0 else nc.vector
+                    eng.tensor_tensor(out=half[:], in0=from_even[:, i, :], in1=from_odd[:, i, :], op=ALU.add)
+                    nc.sync.dma_start(out=dst[i], in_=half[:])
+            if not last:
+                result = res.tile([P, 2, COLS], F32, name="result")
+                nc.gpsimd.tensor_tensor(out=result[:], in0=from_even[:], in1=from_odd[:], op=ALU.add)
+                nc.sync.dma_start(out=dst.rearrange("b p e -> p b e"), in_=result[:])
+
+        make_table(0, 0)
+        x0, q0 = ("x", 0), ("w", 0, 0)
+        transpose_rows(x0, 0)
+        transpose_rows(q0, 0)
+        quantize(x0, 0, 1)
+        transpose_rows(q0, 1)
+        transpose_rows(q0, 2)
+        quantize(q0, 0, 2)
+        transpose_rows(q0, 3)
+        transpose_rows(x0, 1)
+        quantize(q0, 2, 2)
+        transpose_rows(x0, 2)
+        quantize(x0, 1, 1)
+        transpose_rows(x0, 3)
+        multiply(0)
+
+        to_transpose = {1: [(("w", 1, 0), i) for i in range(4)],
+                        2: [(("x", 1), 0), (("x", 1), 1)],
+                        3: [(("x", 1), 2), (("x", 1), 3)]}
+        for i in range(4):
+            to_transpose[4 + i] = [(("x", 2), i), (("w", 0, 1), i)]
+            to_transpose[8 + i] = [(("x", 3), i), (("w", 1, 1), i)]
+        to_quantize = {0: (x0, 2, 2), 1: (("w", 1, 0), 0, 4), 3: (("x", 1), 0, 4), 7: (("x", 2), 0, 4),
+                       8: (("w", 0, 1), 0, 4), 11: (("x", 3), 0, 4), 12: (("w", 1, 1), 0, 4)}
+
+        for s in range(STEPS):
+            if s in to_quantize:
+                quantize(*to_quantize[s])
+            if s + 1 < STEPS:
+                for key, slot in to_transpose.get(s + 1, []):
+                    transpose_rows(key, slot)
+                multiply(s + 1)
+            ahead = s + STEPS_PER_GROUP - 1
+            if s % STEPS_PER_GROUP == 1 and ahead < STEPS:
+                h, j, w, b0 = step_indices(ahead)
+                make_table(h, j)
+            rotate(s)

@@ -21,12 +21,32 @@ ACT = mybir.ActivationFunctionType
 P = 128
 PASSES = 2
 WORDS = 256
-COLS = 512
-PAIRS = 256
+TOKENS = B * P
+BLOCK = 2 * P
 GROUPS = S // P
-HALVES = E // COLS
-STEPS_PER_GROUP = 4
-STEPS = HALVES * GROUPS * STEPS_PER_GROUP
+HALVES = 2
+UNITS_PER_GROUP = 4
+UNITS = HALVES * GROUPS * UNITS_PER_GROUP
+
+
+def unit_indices(s):
+    h, j = s // (GROUPS * UNITS_PER_GROUP), (s // UNITS_PER_GROUP) % GROUPS
+    w, blk = (s % UNITS_PER_GROUP) // 2, s % 2
+    return h, j, w, blk
+
+
+def pairs_on_partitions(s):
+    group, place = divmod(s, UNITS_PER_GROUP)
+    if group == 0:
+        return False
+    if group < 3:
+        return place == 2
+    return place % 2 == 0
+
+
+def gpsimd_multiplies(s):
+    group, place = divmod(s, UNITS_PER_GROUP)
+    return group >= 3 and place == 0
 
 
 def tile_attention_pa_kernel(tc, x, wq, wk, out_0, out_1):
@@ -37,47 +57,48 @@ def tile_attention_pa_kernel(tc, x, wq, wk, out_0, out_1):
     with ExitStack() as ctx:
         keep = ctx.enter_context(tc.tile_pool(name="keep", bufs=1))
         stage = ctx.enter_context(tc.tile_pool(name="stage", bufs=3))
-        work = ctx.enter_context(tc.tile_pool(name="work", bufs=3))
-        res = ctx.enter_context(tc.tile_pool(name="res", bufs=8))
+        small = ctx.enter_context(tc.tile_pool(name="small", bufs=2))
+        tabs = ctx.enter_context(tc.tile_pool(name="tabs", bufs=3))
+        work = ctx.enter_context(tc.tile_pool(name="work", bufs=4))
+        res = ctx.enter_context(tc.tile_pool(name="res", bufs=4))
         tpsum = ctx.enter_context(tc.psum_pool(name="tpsum", bufs=3))
         mpsum = ctx.enter_context(tc.psum_pool(name="mpsum", bufs=5))
         ctx.enter_context(tc.manual_schedule())
 
-        x_raw = {}
-        w_raw = {}
+        raw = {}
 
         def load_x_tile(j, b):
             t = keep.tile([P, D], BF16, name=f"x_raw_{j}_{b}")
             nc.sync.dma_start(out=t[:], in_=x[b, j * P:(j + 1) * P, :])
-            x_raw[(j, b)] = t[:]
+            raw[(("x", j), b)] = t[:]
 
         def load_x_group(j):
             t = keep.tile([P, B, D], BF16, name=f"x_raw_{j}")
             nc.sync.dma_start(out=t[:], in_=x[:, j * P:(j + 1) * P, :].rearrange("b p k -> p b k"))
             for b in range(B):
-                x_raw[(j, b)] = t[:, b, :]
+                raw[(("x", j), b)] = t[:, b, :]
 
-        def load_w_block(w, blk):
-            t = keep.tile([P, 2, D], BF16, name=f"w_raw_{w}_{blk}")
-            rows = weights[w][blk * 2 * P:(blk + 1) * 2 * P, :]
-            nc.sync.dma_start(out=t[:], in_=rows.rearrange("(m two) k -> m two k", two=2))
+        def load_w_block(w, h, blk):
+            t = keep.tile([P, 2, D], BF16, name=f"w_raw_{w}_{h}_{blk}")
+            first = (2 * h + blk) * BLOCK
+            nc.sync.dma_start(out=t[:], in_=weights[w][first:first + BLOCK, :].rearrange("(m two) k -> m two k", two=2))
             for two in range(2):
-                w_raw[(w, blk // 2, (blk % 2) * 2 + two)] = t[:, two, :]
+                raw[(("w", w, h), 2 * blk + two)] = t[:, two, :]
 
         load_x_tile(0, 0)
-        load_w_block(0, 0)
-        load_w_block(0, 1)
+        load_w_block(0, 0, 0)
         for b in range(1, B):
             load_x_tile(0, b)
-        load_w_block(1, 0)
-        load_w_block(1, 1)
+        load_w_block(0, 0, 1)
+        load_w_block(1, 0, 0)
+        load_w_block(1, 0, 1)
         load_x_group(1)
         load_x_group(2)
-        load_w_block(0, 2)
-        load_w_block(0, 3)
+        load_w_block(0, 1, 0)
+        load_w_block(0, 1, 1)
         load_x_group(3)
-        load_w_block(1, 2)
-        load_w_block(1, 3)
+        load_w_block(1, 1, 0)
+        load_w_block(1, 1, 1)
 
         ident = keep.tile([P, P], F32)
         make_identity(nc, ident[:])
@@ -93,148 +114,253 @@ def tile_attention_pa_kernel(tc, x, wq, wk, out_0, out_1):
         nc.vector.tensor_scalar(out=half_pi[:], in0=one[:], scalar1=math.pi / 2.0, scalar2=None, op0=ALU.mult)
         n = 1
         while n < E // 2:
-            nc.vector.tensor_scalar(out=freq[:, n:2 * n], in0=freq[:, 0:n], scalar1=THETA ** (-2.0 * n / E),
-                                    scalar2=None, op0=ALU.mult)
-            n *= 2
+            copies = min(4, E // 2 // n)
+            for c in range(1, copies):
+                nc.vector.tensor_scalar(out=freq[:, c * n:(c + 1) * n], in0=freq[:, 0:n],
+                                        scalar1=THETA ** (-2.0 * c * n / E), scalar2=None, op0=ALU.mult)
+            n *= copies
 
-        whole = keep.tile([P, GROUPS, E // 2], I32)
+        whole = {}
         frac = keep.tile([P, GROUPS, E // 2], F32)
 
         def whole_turns(j):
-            nc.vector.tensor_scalar(out=whole[:, j, :], in0=freq[:], scalar1=pos[:, j:j + 1], scalar2=None, op0=ALU.mult)
+            whole[j] = small.tile([P, E // 2], I32, name="whole")
+            nc.vector.tensor_scalar(out=whole[j][:], in0=freq[:], scalar1=pos[:, j:j + 1], scalar2=None, op0=ALU.mult)
 
         def fraction(j):
-            nc.vector.scalar_tensor_tensor(out=frac[:, j, :], in0=freq[:], scalar=pos[:, j:j + 1], in1=whole[:, j, :],
+            nc.vector.scalar_tensor_tensor(out=frac[:, j, :], in0=freq[:], scalar=pos[:, j:j + 1], in1=whole[j][:],
                                            op0=ALU.mult, op1=ALU.subtract)
-
-        whole_turns(0)
-        for j in range(GROUPS):
-            if j + 1 < GROUPS:
-                whole_turns(j + 1)
-            fraction(j)
 
         tables = {}
 
-        def make_table(h, j):
-            t = keep.tile([P, 3, PAIRS], F32, name=f"table_{h}_{j}")
-            f = frac[:, j, h * PAIRS:(h + 1) * PAIRS]
-            mag = work.tile([P, PAIRS], F32, name="mag")
-            nc.scalar.activation(out=mag[:], in_=f, func=ACT.Abs)
-            nc.scalar.activation(out=t[:, 0, :], in_=f, func=ACT.Sin, scale=-2.0 * math.pi)
-            nc.scalar.activation(out=t[:, 2, :], in_=f, func=ACT.Sin, scale=2.0 * math.pi)
-            nc.scalar.activation(out=t[:, 1, :], in_=mag[:], func=ACT.Sin, scale=-2.0 * math.pi, bias=half_pi[:])
-            tables[(h, j)] = t
+        def fill_table(table, turns, width):
+            mag = small.tile([P, BLOCK], F32, name="mag")
+            nc.scalar.activation(out=mag[:, :width], in_=turns, func=ACT.Abs)
+            nc.scalar.activation(out=table[:, 0, :], in_=turns, func=ACT.Sin, scale=-2.0 * math.pi)
+            nc.scalar.activation(out=table[:, 2, :], in_=turns, func=ACT.Sin, scale=2.0 * math.pi)
+            nc.scalar.activation(out=table[:, 1, :], in_=mag[:, :width], func=ACT.Sin, scale=-2.0 * math.pi,
+                                 bias=half_pi[:])
+
+        def make_token_table(group):
+            h, j = divmod(group, GROUPS)
+            units = range(group * UNITS_PER_GROUP, (group + 1) * UNITS_PER_GROUP)
+            blocks = sorted({s % 2 for s in units if not pairs_on_partitions(s)})
+            width = len(blocks) * P
+            t = tabs.tile([P, 3, width], F32, name="token_table")
+            first = (2 * h + blocks[0]) * P
+            fill_table(t[:], frac[:, j, first:first + width], width)
+            for i, blk in enumerate(blocks):
+                tables[(group, blk, False)] = t[:, :, i * P:(i + 1) * P]
+
+        def make_pair_table(group):
+            h, j = divmod(group, GROUPS)
+            bank = tpsum.tile([P, 4, P], F32, name="tbank")
+            nc.tensor.transpose(bank[:, 0, :], frac[:, j, 2 * h * P:(2 * h + 1) * P], ident[:])
+            t = tabs.tile([P, 3, P], F32, name="pair_table")
+            fill_table(t[:], bank[:, 0, :], P)
+            tables[(group, 0, True)] = t[:]
 
         staged = {}
         codes = {}
         scales = {}
 
         def transpose_rows(key, slot):
-            raw = x_raw[(key[1], slot)] if key[0] == "x" else w_raw[(key[1], key[2], slot)]
+            runs = 1 if key[0] == "x" else 2
+            width = TOKENS // runs
             if slot == 0:
-                staged[key] = stage.tile([P, PASSES, COLS, 4], BF16, name="staged", align_bytes=256)
+                staged[key] = stage.tile([P, runs, PASSES, width * 4], BF16, name="staged", align_bytes=256)
                 name = "_".join(str(v) for v in key)
-                codes[key] = keep.tile([P, PASSES, COLS], U32, name="codes_" + name, align_bytes=256)
-                scales[key] = keep.tile([P, PASSES, COLS], U8, name="scales_" + name, align_bytes=256)
-            words = raw.bitcast(F32)
-            bank = tpsum.tile([P, PASSES, 2, P], F32, name="tbank")
+                codes[key] = keep.tile([P, runs, PASSES, width], U32, name="codes_" + name, align_bytes=256)
+                scales[key] = keep.tile([P, runs, PASSES, width], U8, name="scales_" + name, align_bytes=256)
+            words = raw[(key, slot)].bitcast(F32)
+            bank = tpsum.tile([P, 4, P], F32, name="tbank")
             for g in range(PASSES):
                 for u in range(2):
-                    nc.tensor.transpose(bank[:, g, u, :], words[:, g * WORDS + u:(g + 1) * WORDS:2], ident[:])
-            dst = staged[key][:].rearrange("p g c t -> p g (c t)").bitcast(F32).rearrange("p g (c u) -> p g c u", u=2)
-            nc.scalar.copy(out=dst[:, :, slot * P:(slot + 1) * P, :], in_=bank[:].rearrange("p g u r -> p g r u"))
+                    nc.tensor.transpose(bank[:, 2 * g + u, :], words[:, g * WORDS + u:(g + 1) * WORDS:2], ident[:])
+            run, first = divmod(slot * P, width)
+            dst = staged[key][:, run, :, 4 * first:4 * (first + P)].bitcast(F32).rearrange("p g (c u) -> p g c u", u=2)
+            nc.scalar.copy(out=dst, in_=bank[:].rearrange("p (g u) r -> p g r u", u=2))
 
-        def quantize(key, first, count):
+        def quantize_all(key):
             fmt = E5M2X4 if key[0] == "x" else E4M3X4
-            if count == 4:
-                nc.vector.quantize_mx(out=codes[key][:].rearrange("p g c -> p (g c)").bitcast(fmt),
-                                      scales=scales[key][:].rearrange("p g c -> p (g c)"),
-                                      in_=staged[key][:].rearrange("p g c t -> p (g c t)"))
-                return
-            cols = slice(first * P, (first + count) * P)
-            for g in range(PASSES):
-                nc.vector.quantize_mx(out=codes[key][:, g, cols].bitcast(fmt), scales=scales[key][:, g, cols],
-                                      in_=staged[key][:, g, cols, :].rearrange("p c t -> p (c t)"))
+            nc.vector.quantize_mx(out=codes[key][:].rearrange("p r g c -> p (r g c)").bitcast(fmt),
+                                  scales=scales[key][:].rearrange("p r g c -> p (r g c)"),
+                                  in_=staged[key][:].rearrange("p r g c -> p (r g c)"))
 
-        def step_indices(s):
-            h, j = s // (GROUPS * STEPS_PER_GROUP), (s // STEPS_PER_GROUP) % GROUPS
-            w, b0 = (s % STEPS_PER_GROUP) // 2, 2 * (s % 2)
-            return h, j, w, b0
+        def quantize_w_block(key, blk):
+            nc.vector.quantize_mx(out=codes[key][:, blk].rearrange("p g c -> p (g c)").bitcast(E4M3X4),
+                                  scales=scales[key][:, blk].rearrange("p g c -> p (g c)"),
+                                  in_=staged[key][:, blk].rearrange("p g c -> p (g c)"))
+
+        def quantize_x_tile(key, b):
+            for g in range(PASSES):
+                nc.vector.quantize_mx(out=codes[key][:, 0, g, b * P:(b + 1) * P].bitcast(E5M2X4),
+                                      scales=scales[key][:, 0, g, b * P:(b + 1) * P],
+                                      in_=staged[key][:, 0, g, 4 * b * P:4 * (b + 1) * P])
 
         banks = {}
 
-        def multiply(s):
-            h, j, w, b0 = step_indices(s)
-            xk, wkey = ("x", j), ("w", w, h)
-            for i in range(2):
-                bank = mpsum.tile([P, COLS], F32, name="mbank")
-                cols = slice((b0 + i) * P, (b0 + i + 1) * P)
+        def multiply_bank(s, i):
+            h, j, w, blk = unit_indices(s)
+            xc, xs = codes[("x", j)], scales[("x", j)]
+            wc, ws = codes[("w", w, h)], scales[("w", w, h)]
+            bank = mpsum.tile([P, TOKENS], F32, name="mbank")
+            banks[(s, i)] = bank
+            if pairs_on_partitions(s):
+                cols = slice(i * P, (i + 1) * P)
                 for g in range(PASSES):
-                    nc.tensor.matmul_mx(out=bank[:], lhsT=codes[xk][:, g, cols].bitcast(E5M2X4),
-                                        lhsT_scale=scales[xk][:, g, cols],
-                                        rhs=codes[wkey][:, g, :].bitcast(E4M3X4), rhs_scale=scales[wkey][:, g, :],
+                    nc.tensor.matmul_mx(out=bank[:], lhsT=wc[:, blk, g, cols].bitcast(E4M3X4),
+                                        lhsT_scale=ws[:, blk, g, cols],
+                                        rhs=xc[:, 0, g, :].bitcast(E5M2X4), rhs_scale=xs[:, 0, g, :],
                                         start=(g == 0), stop=(g == PASSES - 1))
-                banks[(s, i)] = bank
+                return
+            for bb in range(2):
+                cols = slice((2 * i + bb) * P, (2 * i + bb + 1) * P)
+                for g in range(PASSES):
+                    nc.tensor.matmul_mx(out=bank[:, bb * BLOCK:(bb + 1) * BLOCK],
+                                        lhsT=xc[:, 0, g, cols].bitcast(E5M2X4), lhsT_scale=xs[:, 0, g, cols],
+                                        rhs=wc[:, blk, g, :].bitcast(E4M3X4), rhs_scale=ws[:, blk, g, :],
+                                        start=(g == 0), stop=(g == PASSES - 1))
 
-        def rotate(s):
-            h, j, w, b0 = step_indices(s)
-            table = tables[(h, j)]
-            from_even = work.tile([P, 2, COLS], F32, name="from_even")
-            from_odd = work.tile([P, 2, COLS], F32, name="from_odd")
-            last = s == STEPS - 1
-            dst = outs[w][b0:b0 + 2, j * P:(j + 1) * P, h * COLS:(h + 1) * COLS]
+        parts = {}
+        results = {}
+
+        def part_tile(s, two):
+            if (s, two) not in parts:
+                parts[(s, two)] = work.tile([P, 2 * TOKENS], F32, name=f"part_{two}")
+            return parts[(s, two)]
+
+        def result_tile(s):
+            if s // 2 not in results:
+                results[s // 2] = res.tile([P, B, 2 * BLOCK], F32, name="result")
+            return results[s // 2]
+
+        def store(s, batches, blocks):
+            h, j, w, blk = unit_indices(s)
+            cols = slice(blocks[0] * BLOCK, (blocks[-1] + 1) * BLOCK)
+            dst = outs[w][batches, j * P:(j + 1) * P, h * 2 * BLOCK:(h + 1) * 2 * BLOCK]
+            nc.sync.dma_start(out=dst[:, :, cols].rearrange("b p e -> p b e"), in_=results[s // 2][:, batches, cols])
+
+        def token_products(s, i):
+            table = tables[(s // UNITS_PER_GROUP, s % 2, False)]
+            u = banks[(s, i)][:].rearrange("p (b two m) -> p b two m", two=2, m=P)
+            for two in range(2):
+                dst = part_tile(s, two)[:, i * TOKENS:(i + 1) * TOKENS]
+                factors = table[:, 1 - two:3 - two, :].rearrange("p c m -> p m c")
+                nc.vector.tensor_tensor(
+                    out=dst.rearrange("p (b m c) -> p b m c", m=P, c=2),
+                    in0=u[:, :, two, :].unsqueeze(3).to_broadcast([P, 2, P, 2]),
+                    in1=factors.unsqueeze(1).to_broadcast([P, 2, P, 2]),
+                    op=ALU.mult)
+
+        def token_sum(s, engine, batches):
+            blk = s % 2
+            views = [parts[(s, two)][:].rearrange("p (b e) -> p b e", b=B)[:, batches, :] for two in range(2)]
+            engine.tensor_tensor(out=result_tile(s)[:, batches, blk * BLOCK:(blk + 1) * BLOCK],
+                                 in0=views[0], in1=views[1], op=ALU.add)
+
+        def pair_products(s, two, engine, source):
+            table = tables[(s // UNITS_PER_GROUP, 0, True)]
+            engine.tensor_tensor(
+                out=part_tile(s, two)[:].rearrange("p (c b t) -> p c b t", c=2, b=B),
+                in0=source.rearrange("p (b t) -> p b t", b=B).unsqueeze(1).to_broadcast([P, 2, B, P]),
+                in1=table[:, 1 - two:3 - two, :].unsqueeze(2).to_broadcast([P, 2, B, P]),
+                op=ALU.mult)
+
+        def odd_products_on_gpsimd(s):
+            odd = small.tile([P, TOKENS], F32, name="odd")
+            nc.scalar.copy(out=odd[:], in_=banks[(s, 1)][:])
+            pair_products(s, 1, nc.gpsimd, odd[:])
+
+        def pair_sums(s):
+            blk = s % 2
+            views = [parts[(s, two)][:].rearrange("p (c b t) -> p c b t", c=2, b=B) for two in range(2)]
             for i in range(2):
-                u = banks[(s, i)][:].rearrange("p (b two m) -> p b two m", two=2, m=P)
-                for two, part, lo in ((0, from_even, 1), (1, from_odd, 0)):
-                    nc.vector.tensor_tensor(
-                        out=part[:, i, :].rearrange("p (b m c) -> p b m c", m=P, c=2),
-                        in0=u[:, :, two, :].unsqueeze(3).to_broadcast([P, 2, P, 2]),
-                        in1=table[:, lo:lo + 2, :].rearrange("p c (b m) -> p b m c", m=P),
-                        op=ALU.mult)
-                if last:
-                    half = res.tile([P, COLS], F32, name="half", bufs=2)
-                    eng = nc.gpsimd if i == 0 else nc.vector
-                    eng.tensor_tensor(out=half[:], in0=from_even[:, i, :], in1=from_odd[:, i, :], op=ALU.add)
-                    nc.sync.dma_start(out=dst[i], in_=half[:])
-            if not last:
-                result = res.tile([P, 2, COLS], F32, name="result")
-                nc.gpsimd.tensor_tensor(out=result[:], in0=from_even[:], in1=from_odd[:], op=ALU.add)
-                nc.sync.dma_start(out=dst.rearrange("b p e -> p b e"), in_=result[:])
+                bank = tpsum.tile([P, 4, P], F32, name="tbank")
+                for bb in range(2):
+                    for c in range(2):
+                        for two in range(2):
+                            nc.tensor.matmul(out=bank[:, 2 * bb + c, :], lhsT=views[two][:, c, 2 * i + bb, :],
+                                             rhs=ident[:], is_transpose=True, start=(two == 0), stop=(two == 1))
+                dst = result_tile(s)[:, 2 * i:2 * i + 2, blk * BLOCK:(blk + 1) * BLOCK]
+                nc.scalar.copy(out=dst.rearrange("p b (m c) -> p b m c", c=2),
+                               in_=bank[:].rearrange("p (b c) m -> p b m c", c=2))
 
-        make_table(0, 0)
-        x0, q0 = ("x", 0), ("w", 0, 0)
+        x0, q0, k0 = ("x", 0), ("w", 0, 0), ("w", 1, 0)
+        whole_turns(0)
+        whole_turns(1)
+        fraction(0)
+        fraction(1)
+        make_token_table(0)
         transpose_rows(x0, 0)
+        whole_turns(2)
+        quantize_x_tile(x0, 0)
+        fraction(2)
         transpose_rows(q0, 0)
-        quantize(x0, 0, 1)
         transpose_rows(q0, 1)
-        transpose_rows(q0, 2)
-        quantize(q0, 0, 2)
-        transpose_rows(q0, 3)
+        whole_turns(3)
+        quantize_w_block(q0, 0)
         transpose_rows(x0, 1)
-        quantize(q0, 2, 2)
+        quantize_x_tile(x0, 1)
+        fraction(3)
         transpose_rows(x0, 2)
-        quantize(x0, 1, 1)
+        multiply_bank(0, 0)
+        quantize_x_tile(x0, 2)
         transpose_rows(x0, 3)
-        multiply(0)
+        transpose_rows(q0, 2)
+        transpose_rows(q0, 3)
+        token_products(0, 0)
+        quantize_x_tile(x0, 3)
+        multiply_bank(0, 1)
+        transpose_rows(k0, 0)
+        transpose_rows(k0, 1)
 
-        to_transpose = {1: [(("w", 1, 0), i) for i in range(4)],
-                        2: [(("x", 1), 0), (("x", 1), 1)],
-                        3: [(("x", 1), 2), (("x", 1), 3)]}
-        for i in range(4):
-            to_transpose[4 + i] = [(("x", 2), i), (("w", 0, 1), i)]
-            to_transpose[8 + i] = [(("x", 3), i), (("w", 1, 1), i)]
-        to_quantize = {0: (x0, 2, 2), 1: (("w", 1, 0), 0, 4), 3: (("x", 1), 0, 4), 7: (("x", 2), 0, 4),
-                       8: (("w", 0, 1), 0, 4), 11: (("x", 3), 0, 4), 12: (("w", 1, 1), 0, 4)}
+        to_transpose = {0: [(k0, 2), (k0, 3)], 1: [(("x", 1), b) for b in range(3)], 2: [(("x", 1), 3)]}
+        queue = [(key, slot) for key in (("x", 2), ("w", 0, 1), ("x", 3), ("w", 1, 1)) for slot in range(4)]
+        s = 3
+        while queue:
+            count = 1 if pairs_on_partitions(s - 1) else 2
+            to_transpose[s], queue = queue[:count], queue[count:]
+            s += 1
+        block_to_quantize = {0: (q0, 1), 1: (k0, 0), 2: (k0, 1)}
+        to_quantize = {3: ("x", 1), 7: ("x", 2), 8: ("w", 0, 1), 11: ("x", 3), 13: ("w", 1, 1)}
 
-        for s in range(STEPS):
+        for s in range(UNITS):
+            group, place = divmod(s, UNITS_PER_GROUP)
+            last = s == UNITS - 1
+            if s in block_to_quantize:
+                quantize_w_block(*block_to_quantize[s])
             if s in to_quantize:
-                quantize(*to_quantize[s])
-            if s + 1 < STEPS:
-                for key, slot in to_transpose.get(s + 1, []):
-                    transpose_rows(key, slot)
-                multiply(s + 1)
-            ahead = s + STEPS_PER_GROUP - 1
-            if s % STEPS_PER_GROUP == 1 and ahead < STEPS:
-                h, j, w, b0 = step_indices(ahead)
-                make_table(h, j)
-            rotate(s)
+                quantize_all(to_quantize[s])
+            if not last:
+                multiply_bank(s + 1, 0)
+                multiply_bank(s + 1, 1)
+                if gpsimd_multiplies(s + 1):
+                    odd_products_on_gpsimd(s + 1)
+            if s > 0 and pairs_on_partitions(s - 1):
+                pair_sums(s - 1)
+                if last:
+                    store(s - 1, slice(0, B), [0])
+            for key, slot in to_transpose.get(s, []):
+                transpose_rows(key, slot)
+            if group + 1 < HALVES * GROUPS:
+                if place == 1:
+                    make_pair_table(group + 1)
+                if place == 2:
+                    make_token_table(group + 1)
+            if pairs_on_partitions(s):
+                pair_products(s, 0, nc.vector, banks[(s, 0)][:])
+                if not gpsimd_multiplies(s):
+                    pair_products(s, 1, nc.vector, banks[(s, 1)][:])
+            elif last:
+                for i, engine in enumerate((nc.gpsimd, nc.vector)):
+                    token_products(s, i)
+                    token_sum(s, engine, slice(2 * i, 2 * i + 2))
+                    store(s, slice(2 * i, 2 * i + 2), [1])
+            else:
+                if s > 0:
+                    token_products(s, 0)
+                token_products(s, 1)
+                token_sum(s, nc.gpsimd, slice(0, B))
+                if s % 2 == 1:
+                    store(s, slice(0, B), [0, 1])

@@ -26,6 +26,7 @@ BLOCK = 2 * P
 GROUPS = S // P
 HALVES = 2
 UNITS_PER_GROUP = 4
+HELD_BACK = 16
 UNITS = HALVES * GROUPS * UNITS_PER_GROUP
 
 
@@ -241,17 +242,21 @@ def tile_attention_pa_kernel(tc, x, wq, wk, out_0, out_1):
             dst = outs[w][batches, j * P:(j + 1) * P, h * 2 * BLOCK:(h + 1) * 2 * BLOCK]
             nc.sync.dma_start(out=dst[:, :, cols].rearrange("b p e -> p b e"), in_=results[s // 2][:, batches, cols])
 
-        def token_products(s, i):
+        def token_product(s, i, two, first=0, count=P):
             table = tables[(s // UNITS_PER_GROUP, s % 2, False)]
             u = banks[(s, i)][:].rearrange("p (b two m) -> p b two m", two=2, m=P)
+            pairs = slice(first, first + count)
+            dst = part_tile(s, two)[:, i * TOKENS:(i + 1) * TOKENS]
+            factors = table[:, 1 - two:3 - two, pairs].rearrange("p c m -> p m c")
+            nc.vector.tensor_tensor(
+                out=dst.rearrange("p (b m c) -> p b m c", m=P, c=2)[:, :, pairs, :],
+                in0=u[:, :, two, pairs].unsqueeze(3).to_broadcast([P, 2, count, 2]),
+                in1=factors.unsqueeze(1).to_broadcast([P, 2, count, 2]),
+                op=ALU.mult)
+
+        def token_products(s, i):
             for two in range(2):
-                dst = part_tile(s, two)[:, i * TOKENS:(i + 1) * TOKENS]
-                factors = table[:, 1 - two:3 - two, :].rearrange("p c m -> p m c")
-                nc.vector.tensor_tensor(
-                    out=dst.rearrange("p (b m c) -> p b m c", m=P, c=2),
-                    in0=u[:, :, two, :].unsqueeze(3).to_broadcast([P, 2, P, 2]),
-                    in1=factors.unsqueeze(1).to_broadcast([P, 2, P, 2]),
-                    op=ALU.mult)
+                token_product(s, i, two)
 
         def token_sum(s, engine, batches):
             blk = s % 2
@@ -315,23 +320,23 @@ def tile_attention_pa_kernel(tc, x, wq, wk, out_0, out_1):
         transpose_rows(k0, 0)
         transpose_rows(k0, 1)
 
-        to_transpose = {0: [(k0, 2), (k0, 3)], 1: [(("x", 1), b) for b in range(3)], 2: [(("x", 1), 3)]}
+        to_transpose = {0: [(k0, 2), (k0, 3)], 1: [(("x", 1), b) for b in range(B)]}
         queue = [(key, slot) for key in (("x", 2), ("w", 0, 1), ("x", 3), ("w", 1, 1)) for slot in range(4)]
-        s = 3
+        s = 2
         while queue:
             count = 1 if pairs_on_partitions(s - 1) else 2
             to_transpose[s], queue = queue[:count], queue[count:]
             s += 1
-        block_to_quantize = {0: (q0, 1), 1: (k0, 0), 2: (k0, 1)}
-        to_quantize = {3: ("x", 1), 7: ("x", 2), 8: ("w", 0, 1), 11: ("x", 3), 13: ("w", 1, 1)}
+        quantize_w_block(q0, 1)
+        inside_unit = {0: lambda: quantize_w_block(k0, 0), 1: lambda: quantize_w_block(k0, 1),
+                       2: lambda: quantize_all(("x", 1))}
+        to_quantize = {7: [("x", 2)], 11: [("x", 3), ("w", 0, 1)], 15: [("w", 1, 1)]}
 
         for s in range(UNITS):
             group, place = divmod(s, UNITS_PER_GROUP)
             last = s == UNITS - 1
-            if s in block_to_quantize:
-                quantize_w_block(*block_to_quantize[s])
-            if s in to_quantize:
-                quantize_all(to_quantize[s])
+            for key in to_quantize.get(s, []):
+                quantize_all(key)
             if not last:
                 multiply_bank(s + 1, 0)
                 multiply_bank(s + 1, 1)
@@ -360,7 +365,13 @@ def tile_attention_pa_kernel(tc, x, wq, wk, out_0, out_1):
             else:
                 if s > 0:
                     token_products(s, 0)
-                token_products(s, 1)
+                if s in inside_unit:
+                    token_product(s, 1, 0)
+                    token_product(s, 1, 1, 0, P - HELD_BACK)
+                    inside_unit[s]()
+                    token_product(s, 1, 1, P - HELD_BACK, HELD_BACK)
+                else:
+                    token_products(s, 1)
                 token_sum(s, nc.gpsimd, slice(0, B))
                 if s % 2 == 1:
                     store(s, slice(0, B), [0, 1])

@@ -61,7 +61,7 @@ def tile_attention_pa_kernel(tc, x, wq, wk, out_0, out_1):
         small = ctx.enter_context(tc.tile_pool(name="small", bufs=2))
         tabs = ctx.enter_context(tc.tile_pool(name="tabs", bufs=3))
         work = ctx.enter_context(tc.tile_pool(name="work", bufs=4))
-        res = ctx.enter_context(tc.tile_pool(name="res", bufs=4))
+        res = ctx.enter_context(tc.tile_pool(name="res", bufs=3))
         tpsum = ctx.enter_context(tc.psum_pool(name="tpsum", bufs=3))
         mpsum = ctx.enter_context(tc.psum_pool(name="mpsum", bufs=5))
         ctx.enter_context(tc.manual_schedule())
@@ -101,36 +101,43 @@ def tile_attention_pa_kernel(tc, x, wq, wk, out_0, out_1):
         load_w_block(1, 1, 0)
         load_w_block(1, 1, 1)
 
-        ident = keep.tile([P, P], F32)
-        make_identity(nc, ident[:])
         pos = keep.tile([P, GROUPS], F32)
         nc.gpsimd.iota(pos[:], pattern=[[P, GROUPS]], base=0, channel_multiplier=1,
                        allow_small_or_imprecise_dtypes=True)
+        ident = keep.tile([P, P], F32)
+        make_identity(nc, ident[:])
 
         one = keep.tile([P, 1], F32)
         nc.vector.memset(one[:], 1.0)
         freq = keep.tile([P, E // 2], F32)
         half_pi = keep.tile([P, 1], F32)
-        nc.vector.tensor_scalar(out=freq[:, 0:1], in0=one[:], scalar1=1.0 / (2.0 * math.pi), scalar2=None, op0=ALU.mult)
-        nc.vector.tensor_scalar(out=half_pi[:], in0=one[:], scalar1=math.pi / 2.0, scalar2=None, op0=ALU.mult)
-        n = 1
-        while n < E // 2:
-            copies = min(4, E // 2 // n)
+
+        def extend_freq(n, copies):
             for c in range(1, copies):
                 nc.vector.tensor_scalar(out=freq[:, c * n:(c + 1) * n], in0=freq[:, 0:n],
                                         scalar1=THETA ** (-2.0 * c * n / E), scalar2=None, op0=ALU.mult)
-            n *= copies
+
+        for c in range(4):
+            nc.vector.tensor_scalar(out=freq[:, c:c + 1], in0=one[:], scalar1=THETA ** (-2.0 * c / E) / (2.0 * math.pi),
+                                    scalar2=None, op0=ALU.mult)
+        nc.vector.tensor_scalar(out=half_pi[:], in0=one[:], scalar1=math.pi / 2.0, scalar2=None, op0=ALU.mult)
+        extend_freq(4, 4)
+        extend_freq(16, 4)
+        extend_freq(64, 2)
 
         whole = {}
-        frac = keep.tile([P, GROUPS, E // 2], F32)
+        signed = keep.tile([P, GROUPS, 2, E // 2], F32)
+        frac = signed[:, :, 1, :]
 
-        def whole_turns(j):
-            whole[j] = small.tile([P, E // 2], I32, name="whole")
-            nc.vector.tensor_scalar(out=whole[j][:], in0=freq[:], scalar1=pos[:, j:j + 1], scalar2=None, op0=ALU.mult)
+        def whole_turns(j, pairs=slice(0, E // 2)):
+            if j not in whole:
+                whole[j] = small.tile([P, E // 2], I32, name="whole")
+            nc.vector.tensor_scalar(out=whole[j][:, pairs], in0=freq[:, pairs], scalar1=pos[:, j:j + 1], scalar2=None,
+                                    op0=ALU.mult)
 
-        def fraction(j):
-            nc.vector.scalar_tensor_tensor(out=frac[:, j, :], in0=freq[:], scalar=pos[:, j:j + 1], in1=whole[j][:],
-                                           op0=ALU.mult, op1=ALU.subtract)
+        def fraction(j, pairs=slice(0, E // 2)):
+            nc.vector.scalar_tensor_tensor(out=frac[:, j, pairs], in0=freq[:, pairs], scalar=pos[:, j:j + 1],
+                                           in1=whole[j][:, pairs], op0=ALU.mult, op1=ALU.subtract)
 
         tables = {}
 
@@ -142,16 +149,24 @@ def tile_attention_pa_kernel(tc, x, wq, wk, out_0, out_1):
             nc.scalar.activation(out=table[:, 1, :], in_=mag[:, :width], func=ACT.Sin, scale=-2.0 * math.pi,
                                  bias=half_pi[:])
 
-        def make_token_table(group):
-            h, j = divmod(group, GROUPS)
+        def token_blocks(group):
             units = range(group * UNITS_PER_GROUP, (group + 1) * UNITS_PER_GROUP)
-            blocks = sorted({s % 2 for s in units if not pairs_on_partitions(s)})
+            return sorted({s % 2 for s in units if not pairs_on_partitions(s)})
+
+        def make_token_table(group, blocks):
+            h, j = divmod(group, GROUPS)
             width = len(blocks) * P
-            t = tabs.tile([P, 3, width], F32, name="token_table")
-            first = (2 * h + blocks[0]) * P
-            fill_table(t[:], frac[:, j, first:first + width], width)
+            t = tabs.tile([P, 2, width, 2], F32, name="token_table")
+            pairs = slice((2 * h + blocks[0]) * P, (2 * h + blocks[0]) * P + width)
+            mag = small.tile([P, BLOCK], F32, name="mag")
+            nc.scalar.activation(out=mag[:, :width], in_=frac[:, j, pairs], func=ACT.Abs)
+            nc.scalar.activation(out=signed[:, j, 0, pairs], in_=frac[:, j, pairs], func=ACT.Copy, scale=-1.0)
+            nc.scalar.activation(out=t[:, 0], in_=mag[:, :width].unsqueeze(2).to_broadcast([P, width, 2]),
+                                 func=ACT.Sin, scale=-2.0 * math.pi, bias=half_pi[:])
+            nc.scalar.activation(out=t[:, 1], in_=signed[:, j, :, pairs].rearrange("p c m -> p m c"),
+                                 func=ACT.Sin, scale=2.0 * math.pi)
             for i, blk in enumerate(blocks):
-                tables[(group, blk, False)] = t[:, :, i * P:(i + 1) * P]
+                tables[(group, blk, False)] = t[:, :, i * P:(i + 1) * P, :]
 
         def make_pair_table(group):
             h, j = divmod(group, GROUPS)
@@ -247,11 +262,11 @@ def tile_attention_pa_kernel(tc, x, wq, wk, out_0, out_1):
             u = banks[(s, i)][:].rearrange("p (b two m) -> p b two m", two=2, m=P)
             pairs = slice(first, first + count)
             dst = part_tile(s, two)[:, i * TOKENS:(i + 1) * TOKENS]
-            factors = table[:, 1 - two:3 - two, pairs].rearrange("p c m -> p m c")
+            halves = u[:, :, :, pairs] if two == 0 else u[:, :, ::-1, pairs]
             nc.vector.tensor_tensor(
                 out=dst.rearrange("p (b m c) -> p b m c", m=P, c=2)[:, :, pairs, :],
-                in0=u[:, :, two, pairs].unsqueeze(3).to_broadcast([P, 2, count, 2]),
-                in1=factors.unsqueeze(1).to_broadcast([P, 2, count, 2]),
+                in0=halves.rearrange("p b c m -> p b m c"),
+                in1=table[:, two, pairs, :].unsqueeze(1).to_broadcast([P, 2, count, 2]),
                 op=ALU.mult)
 
         def token_products(s, i):
@@ -292,11 +307,14 @@ def tile_attention_pa_kernel(tc, x, wq, wk, out_0, out_1):
                                in_=bank[:].rearrange("p (b c) m -> p b m c", c=2))
 
         x0, q0, k0 = ("x", 0), ("w", 0, 0), ("w", 1, 0)
-        whole_turns(0)
+        whole_turns(0, slice(0, P))
+        extend_freq(P, 4)
+        fraction(0, slice(0, P))
+        make_token_table(0, [0])
+        whole_turns(0, slice(P, E // 2))
         whole_turns(1)
-        fraction(0)
+        fraction(0, slice(P, E // 2))
         fraction(1)
-        make_token_table(0)
         transpose_rows(x0, 0)
         whole_turns(2)
         quantize_x_tile(x0, 0)
@@ -310,6 +328,7 @@ def tile_attention_pa_kernel(tc, x, wq, wk, out_0, out_1):
         fraction(3)
         transpose_rows(x0, 2)
         multiply_bank(0, 0)
+        make_token_table(0, [1])
         quantize_x_tile(x0, 2)
         transpose_rows(x0, 3)
         transpose_rows(q0, 2)
@@ -352,7 +371,7 @@ def tile_attention_pa_kernel(tc, x, wq, wk, out_0, out_1):
                 if place == 1:
                     make_pair_table(group + 1)
                 if place == 2:
-                    make_token_table(group + 1)
+                    make_token_table(group + 1, token_blocks(group + 1))
             if pairs_on_partitions(s):
                 pair_products(s, 0, nc.vector, banks[(s, 0)][:])
                 if not gpsimd_multiplies(s):

@@ -19,35 +19,39 @@ ALU = mybir.AluOpType
 ACT = mybir.ActivationFunctionType
 
 P = 128
-PASSES = 2
-WORDS = 256
+PACK = 4
+PASSES = D // (P * PACK)
+PASS_PAIRS = P * PACK // 2
+PAIRS = E // 2
 TOKENS = B * P
 BLOCK = 2 * P
-GROUPS = S // P
-HALVES = 2
-UNITS_PER_GROUP = 4
+POSITION_GROUPS = S // P
+SLOTS = 4
+UNITS_PER_ROUND = 4
+ROUNDS = 2 * POSITION_GROUPS
+UNITS = ROUNDS * UNITS_PER_ROUND
+
+FIRST_PAIR_UNIT = 10
+GPSIMD_SHARE = 3
+SLOTS_PER_STEP = 2
 HELD_BACK = 16
-UNITS = HALVES * GROUPS * UNITS_PER_GROUP
+QUANTIZE_AFTER = {("x", 2): 6, ("x", 3): 10, ("w", 0, 1): 10, ("w", 1, 1): 14}
 
 
 def unit_indices(s):
-    h, j = s // (GROUPS * UNITS_PER_GROUP), (s // UNITS_PER_GROUP) % GROUPS
-    w, blk = (s % UNITS_PER_GROUP) // 2, s % 2
-    return h, j, w, blk
+    half, group = divmod(s // UNITS_PER_ROUND, POSITION_GROUPS)
+    proj, blk = divmod(s % UNITS_PER_ROUND, 2)
+    return half, group, proj, blk
 
 
-def pairs_on_partitions(s):
-    group, place = divmod(s, UNITS_PER_GROUP)
-    if group == 0:
-        return False
-    if group < 3:
-        return place == 2
-    return place % 2 == 0
+def is_pair_unit(s):
+    return s >= FIRST_PAIR_UNIT and s % 2 == 0
 
 
-def gpsimd_multiplies(s):
-    group, place = divmod(s, UNITS_PER_GROUP)
-    return group >= 3 and place == 0
+def gpsimd_batches(s):
+    if not is_pair_unit(s) or s in QUANTIZE_AFTER.values() or s == UNITS - 2:
+        return 0
+    return GPSIMD_SHARE
 
 
 def tile_attention_pa_kernel(tc, x, wq, wk, out_0, out_1):
@@ -68,28 +72,29 @@ def tile_attention_pa_kernel(tc, x, wq, wk, out_0, out_1):
 
         raw = {}
 
-        def load_x_tile(j, b):
-            t = keep.tile([P, D], BF16, name=f"x_raw_{j}_{b}")
-            nc.sync.dma_start(out=t[:], in_=x[b, j * P:(j + 1) * P, :])
-            raw[(("x", j), b)] = t[:]
+        def load_x_slot(group, b):
+            rows = keep.tile([P, D], BF16, name=f"x_raw_{group}_{b}")
+            nc.sync.dma_start(out=rows[:], in_=x[b, group * P:(group + 1) * P, :])
+            raw[(("x", group), b)] = rows[:]
 
-        def load_x_group(j):
-            t = keep.tile([P, B, D], BF16, name=f"x_raw_{j}")
-            nc.sync.dma_start(out=t[:], in_=x[:, j * P:(j + 1) * P, :].rearrange("b p k -> p b k"))
+        def load_x_group(group):
+            rows = keep.tile([P, B, D], BF16, name=f"x_raw_{group}")
+            nc.sync.dma_start(out=rows[:], in_=x[:, group * P:(group + 1) * P, :].rearrange("b p k -> p b k"))
             for b in range(B):
-                raw[(("x", j), b)] = t[:, b, :]
+                raw[(("x", group), b)] = rows[:, b, :]
 
-        def load_w_block(w, h, blk):
-            t = keep.tile([P, 2, D], BF16, name=f"w_raw_{w}_{h}_{blk}")
-            first = (2 * h + blk) * BLOCK
-            nc.sync.dma_start(out=t[:], in_=weights[w][first:first + BLOCK, :].rearrange("(m two) k -> m two k", two=2))
-            for two in range(2):
-                raw[(("w", w, h), 2 * blk + two)] = t[:, two, :]
+        def load_w_block(proj, half, blk):
+            rows = keep.tile([P, 2, D], BF16, name=f"w_raw_{proj}_{half}_{blk}")
+            first = (2 * half + blk) * BLOCK
+            src = weights[proj][first:first + BLOCK, :].rearrange("(m odd) k -> m odd k", odd=2)
+            nc.sync.dma_start(out=rows[:], in_=src)
+            for odd in range(2):
+                raw[(("w", proj, half), 2 * blk + odd)] = rows[:, odd, :]
 
-        load_x_tile(0, 0)
+        load_x_slot(0, 0)
         load_w_block(0, 0, 0)
         for b in range(1, B):
-            load_x_tile(0, b)
+            load_x_slot(0, b)
         load_w_block(0, 0, 1)
         load_w_block(1, 0, 0)
         load_w_block(1, 0, 1)
@@ -101,21 +106,21 @@ def tile_attention_pa_kernel(tc, x, wq, wk, out_0, out_1):
         load_w_block(1, 1, 0)
         load_w_block(1, 1, 1)
 
-        pos = keep.tile([P, GROUPS], F32)
-        nc.gpsimd.iota(pos[:], pattern=[[P, GROUPS]], base=0, channel_multiplier=1,
+        position = keep.tile([P, POSITION_GROUPS], F32)
+        nc.gpsimd.iota(position[:], pattern=[[P, POSITION_GROUPS]], base=0, channel_multiplier=1,
                        allow_small_or_imprecise_dtypes=True)
         ident = keep.tile([P, P], F32)
         make_identity(nc, ident[:])
 
         one = keep.tile([P, 1], F32)
         nc.vector.memset(one[:], 1.0)
-        freq = keep.tile([P, E // 2], F32)
+        freq = keep.tile([P, PAIRS], F32)
         half_pi = keep.tile([P, 1], F32)
 
-        def extend_freq(n, copies):
-            for c in range(1, copies):
-                nc.vector.tensor_scalar(out=freq[:, c * n:(c + 1) * n], in0=freq[:, 0:n],
-                                        scalar1=THETA ** (-2.0 * c * n / E), scalar2=None, op0=ALU.mult)
+        def extend_freq(known, factor):
+            for c in range(1, factor):
+                nc.vector.tensor_scalar(out=freq[:, c * known:(c + 1) * known], in0=freq[:, 0:known],
+                                        scalar1=THETA ** (-2.0 * c * known / E), scalar2=None, op0=ALU.mult)
 
         for c in range(4):
             nc.vector.tensor_scalar(out=freq[:, c:c + 1], in0=one[:], scalar1=THETA ** (-2.0 * c / E) / (2.0 * math.pi),
@@ -126,78 +131,71 @@ def tile_attention_pa_kernel(tc, x, wq, wk, out_0, out_1):
         extend_freq(64, 2)
 
         whole = {}
-        signed = keep.tile([P, GROUPS, 2, E // 2], F32)
-        frac = signed[:, :, 1, :]
+        frac = keep.tile([P, POSITION_GROUPS, PAIRS], F32)
 
-        def whole_turns(j, pairs=slice(0, E // 2)):
-            if j not in whole:
-                whole[j] = small.tile([P, E // 2], I32, name="whole")
-            nc.vector.tensor_scalar(out=whole[j][:, pairs], in0=freq[:, pairs], scalar1=pos[:, j:j + 1], scalar2=None,
-                                    op0=ALU.mult)
+        def whole_turns(group, pairs):
+            if group not in whole:
+                whole[group] = small.tile([P, PAIRS], I32, name="whole")
+            nc.vector.tensor_scalar(out=whole[group][:, pairs], in0=freq[:, pairs],
+                                    scalar1=position[:, group:group + 1], scalar2=None, op0=ALU.mult)
 
-        def fraction(j, pairs=slice(0, E // 2)):
-            nc.vector.scalar_tensor_tensor(out=frac[:, j, pairs], in0=freq[:, pairs], scalar=pos[:, j:j + 1],
-                                           in1=whole[j][:, pairs], op0=ALU.mult, op1=ALU.subtract)
+        def fraction(group, pairs):
+            nc.vector.scalar_tensor_tensor(out=frac[:, group, pairs], in0=freq[:, pairs],
+                                           scalar=position[:, group:group + 1], in1=whole[group][:, pairs],
+                                           op0=ALU.mult, op1=ALU.subtract)
 
-        tables = {}
+        token_tables = {}
+        pair_tables = {}
 
         def fill_table(table, turns, width):
-            mag = small.tile([P, BLOCK], F32, name="mag")
-            nc.scalar.activation(out=mag[:, :width], in_=turns, func=ACT.Abs)
+            size = small.tile([P, BLOCK], F32, name="size")
+            nc.scalar.activation(out=size[:, :width], in_=turns, func=ACT.Abs)
             nc.scalar.activation(out=table[:, 0, :], in_=turns, func=ACT.Sin, scale=-2.0 * math.pi)
             nc.scalar.activation(out=table[:, 2, :], in_=turns, func=ACT.Sin, scale=2.0 * math.pi)
-            nc.scalar.activation(out=table[:, 1, :], in_=mag[:, :width], func=ACT.Sin, scale=-2.0 * math.pi,
+            nc.scalar.activation(out=table[:, 1, :], in_=size[:, :width], func=ACT.Sin, scale=-2.0 * math.pi,
                                  bias=half_pi[:])
 
-        def token_blocks(group):
-            units = range(group * UNITS_PER_GROUP, (group + 1) * UNITS_PER_GROUP)
-            return sorted({s % 2 for s in units if not pairs_on_partitions(s)})
-
-        def make_token_table(group, blocks):
-            h, j = divmod(group, GROUPS)
+        def make_token_table(rnd, blocks):
+            half, group = divmod(rnd, POSITION_GROUPS)
             width = len(blocks) * P
-            t = tabs.tile([P, 2, width, 2], F32, name="token_table")
-            pairs = slice((2 * h + blocks[0]) * P, (2 * h + blocks[0]) * P + width)
-            mag = small.tile([P, BLOCK], F32, name="mag")
-            nc.scalar.activation(out=mag[:, :width], in_=frac[:, j, pairs], func=ACT.Abs)
-            nc.scalar.activation(out=signed[:, j, 0, pairs], in_=frac[:, j, pairs], func=ACT.Copy, scale=-1.0)
-            nc.scalar.activation(out=t[:, 0], in_=mag[:, :width].unsqueeze(2).to_broadcast([P, width, 2]),
-                                 func=ACT.Sin, scale=-2.0 * math.pi, bias=half_pi[:])
-            nc.scalar.activation(out=t[:, 1], in_=signed[:, j, :, pairs].rearrange("p c m -> p m c"),
-                                 func=ACT.Sin, scale=2.0 * math.pi)
+            table = tabs.tile([P, 3, width], F32, name="token_table")
+            first = (2 * half + blocks[0]) * P
+            fill_table(table[:], frac[:, group, first:first + width], width)
             for i, blk in enumerate(blocks):
-                tables[(group, blk, False)] = t[:, :, i * P:(i + 1) * P, :]
+                token_tables[(rnd, blk)] = table[:, :, i * P:(i + 1) * P]
 
-        def make_pair_table(group):
-            h, j = divmod(group, GROUPS)
+        def make_pair_table(rnd):
+            half, group = divmod(rnd, POSITION_GROUPS)
             bank = tpsum.tile([P, 4, P], F32, name="tbank")
-            nc.tensor.transpose(bank[:, 0, :], frac[:, j, 2 * h * P:(2 * h + 1) * P], ident[:])
-            t = tabs.tile([P, 3, P], F32, name="pair_table")
-            fill_table(t[:], bank[:, 0, :], P)
-            tables[(group, 0, True)] = t[:]
+            nc.tensor.transpose(bank[:, 0, :], frac[:, group, 2 * half * P:(2 * half + 1) * P], ident[:])
+            table = tabs.tile([P, 3, P], F32, name="pair_table")
+            fill_table(table[:], bank[:, 0, :], P)
+            pair_tables[rnd] = table[:]
 
         staged = {}
         codes = {}
         scales = {}
 
-        def transpose_rows(key, slot):
+        def transpose_slot(key, slot):
             runs = 1 if key[0] == "x" else 2
-            width = TOKENS // runs
+            width = SLOTS * P // runs
             if slot == 0:
-                staged[key] = stage.tile([P, runs, PASSES, width * 4], BF16, name="staged", align_bytes=256)
-                name = "_".join(str(v) for v in key)
-                codes[key] = keep.tile([P, runs, PASSES, width], U32, name="codes_" + name, align_bytes=256)
-                scales[key] = keep.tile([P, runs, PASSES, width], U8, name="scales_" + name, align_bytes=256)
-            words = raw[(key, slot)].bitcast(F32)
+                staged[key] = stage.tile([P, runs, PASSES, width * PACK], BF16, name="staged", align_bytes=256)
+                suffix = "_".join(str(v) for v in key)
+                codes[key] = keep.tile([P, runs, PASSES, width], U32, name="codes_" + suffix, align_bytes=256)
+                scales[key] = keep.tile([P, runs, PASSES, width], U8, name="scales_" + suffix, align_bytes=256)
+            k_pairs = raw[(key, slot)].bitcast(F32)
             bank = tpsum.tile([P, 4, P], F32, name="tbank")
             for g in range(PASSES):
                 for u in range(2):
-                    nc.tensor.transpose(bank[:, 2 * g + u, :], words[:, g * WORDS + u:(g + 1) * WORDS:2], ident[:])
+                    nc.tensor.transpose(bank[:, 2 * g + u, :], k_pairs[:, g * PASS_PAIRS + u:(g + 1) * PASS_PAIRS:2],
+                                        ident[:])
             run, first = divmod(slot * P, width)
-            dst = staged[key][:, run, :, 4 * first:4 * (first + P)].bitcast(F32).rearrange("p g (c u) -> p g c u", u=2)
-            nc.scalar.copy(out=dst, in_=bank[:].rearrange("p (g u) r -> p g r u", u=2))
+            dst = staged[key][:, run, :, PACK * first:PACK * (first + P)].bitcast(F32)
+            nc.scalar.copy(out=dst.rearrange("p g (c u) -> p g c u", u=2),
+                           in_=bank[:].rearrange("p (g u) c -> p g c u", u=2))
 
-        def quantize_all(key):
+        def quantize_operand(key):
             fmt = E5M2X4 if key[0] == "x" else E4M3X4
             nc.vector.quantize_mx(out=codes[key][:].rearrange("p r g c -> p (r g c)").bitcast(fmt),
                                   scales=scales[key][:].rearrange("p r g c -> p (r g c)"),
@@ -208,43 +206,45 @@ def tile_attention_pa_kernel(tc, x, wq, wk, out_0, out_1):
                                   scales=scales[key][:, blk].rearrange("p g c -> p (g c)"),
                                   in_=staged[key][:, blk].rearrange("p g c -> p (g c)"))
 
-        def quantize_x_tile(key, b):
+        def quantize_x_slot(key, b):
             for g in range(PASSES):
                 nc.vector.quantize_mx(out=codes[key][:, 0, g, b * P:(b + 1) * P].bitcast(E5M2X4),
                                       scales=scales[key][:, 0, g, b * P:(b + 1) * P],
-                                      in_=staged[key][:, 0, g, 4 * b * P:4 * (b + 1) * P])
+                                      in_=staged[key][:, 0, g, PACK * b * P:PACK * (b + 1) * P])
 
         banks = {}
 
         def multiply_bank(s, i):
-            h, j, w, blk = unit_indices(s)
-            xc, xs = codes[("x", j)], scales[("x", j)]
-            wc, ws = codes[("w", w, h)], scales[("w", w, h)]
+            half, group, proj, blk = unit_indices(s)
+            x_codes, x_scales = codes[("x", group)], scales[("x", group)]
+            w_codes, w_scales = codes[("w", proj, half)], scales[("w", proj, half)]
             bank = mpsum.tile([P, TOKENS], F32, name="mbank")
             banks[(s, i)] = bank
-            if pairs_on_partitions(s):
+            if is_pair_unit(s):
                 cols = slice(i * P, (i + 1) * P)
                 for g in range(PASSES):
-                    nc.tensor.matmul_mx(out=bank[:], lhsT=wc[:, blk, g, cols].bitcast(E4M3X4),
-                                        lhsT_scale=ws[:, blk, g, cols],
-                                        rhs=xc[:, 0, g, :].bitcast(E5M2X4), rhs_scale=xs[:, 0, g, :],
+                    nc.tensor.matmul_mx(out=bank[:], lhsT=w_codes[:, blk, g, cols].bitcast(E4M3X4),
+                                        lhsT_scale=w_scales[:, blk, g, cols],
+                                        rhs=x_codes[:, 0, g, :].bitcast(E5M2X4), rhs_scale=x_scales[:, 0, g, :],
                                         start=(g == 0), stop=(g == PASSES - 1))
-                return
-            for bb in range(2):
-                cols = slice((2 * i + bb) * P, (2 * i + bb + 1) * P)
-                for g in range(PASSES):
-                    nc.tensor.matmul_mx(out=bank[:, bb * BLOCK:(bb + 1) * BLOCK],
-                                        lhsT=xc[:, 0, g, cols].bitcast(E5M2X4), lhsT_scale=xs[:, 0, g, cols],
-                                        rhs=wc[:, blk, g, :].bitcast(E4M3X4), rhs_scale=ws[:, blk, g, :],
-                                        start=(g == 0), stop=(g == PASSES - 1))
+            else:
+                for bb in range(2):
+                    cols = slice((2 * i + bb) * P, (2 * i + bb + 1) * P)
+                    for g in range(PASSES):
+                        nc.tensor.matmul_mx(out=bank[:, bb * BLOCK:(bb + 1) * BLOCK],
+                                            lhsT=x_codes[:, 0, g, cols].bitcast(E5M2X4),
+                                            lhsT_scale=x_scales[:, 0, g, cols],
+                                            rhs=w_codes[:, blk, g, :].bitcast(E4M3X4),
+                                            rhs_scale=w_scales[:, blk, g, :],
+                                            start=(g == 0), stop=(g == PASSES - 1))
 
-        parts = {}
+        products = {}
         results = {}
 
-        def part_tile(s, two):
-            if (s, two) not in parts:
-                parts[(s, two)] = work.tile([P, 2 * TOKENS], F32, name=f"part_{two}")
-            return parts[(s, two)]
+        def product_tile(s, odd):
+            if (s, odd) not in products:
+                products[(s, odd)] = work.tile([P, 2 * TOKENS], F32, name=f"products_{odd}")
+            return products[(s, odd)]
 
         def result_tile(s):
             if s // 2 not in results:
@@ -252,131 +252,140 @@ def tile_attention_pa_kernel(tc, x, wq, wk, out_0, out_1):
             return results[s // 2]
 
         def store(s, batches, blocks):
-            h, j, w, blk = unit_indices(s)
+            half, group, proj, blk = unit_indices(s)
             cols = slice(blocks[0] * BLOCK, (blocks[-1] + 1) * BLOCK)
-            dst = outs[w][batches, j * P:(j + 1) * P, h * 2 * BLOCK:(h + 1) * 2 * BLOCK]
+            dst = outs[proj][batches, group * P:(group + 1) * P, half * 2 * BLOCK:(half + 1) * 2 * BLOCK]
             nc.sync.dma_start(out=dst[:, :, cols].rearrange("b p e -> p b e"), in_=results[s // 2][:, batches, cols])
 
-        def token_product(s, i, two, first=0, count=P):
-            table = tables[(s // UNITS_PER_GROUP, s % 2, False)]
-            u = banks[(s, i)][:].rearrange("p (b two m) -> p b two m", two=2, m=P)
+        def token_product(s, i, odd, first, count):
+            u = banks[(s, i)][:].rearrange("p (b odd m) -> p b odd m", odd=2, m=P)
             pairs = slice(first, first + count)
-            dst = part_tile(s, two)[:, i * TOKENS:(i + 1) * TOKENS]
-            halves = u[:, :, :, pairs] if two == 0 else u[:, :, ::-1, pairs]
-            nc.vector.tensor_tensor(
-                out=dst.rearrange("p (b m c) -> p b m c", m=P, c=2)[:, :, pairs, :],
-                in0=halves.rearrange("p b c m -> p b m c"),
-                in1=table[:, two, pairs, :].unsqueeze(1).to_broadcast([P, 2, count, 2]),
-                op=ALU.mult)
+            dst = product_tile(s, odd)[:, i * TOKENS:(i + 1) * TOKENS]
+            factors = token_tables[(s // UNITS_PER_ROUND, s % 2)][:, 1 - odd:3 - odd, pairs].rearrange("p c m -> p m c")
+            nc.vector.tensor_tensor(out=dst.rearrange("p (b m c) -> p b m c", m=P, c=2)[:, :, pairs, :],
+                                    in0=u[:, :, odd, pairs].unsqueeze(3).to_broadcast([P, 2, count, 2]),
+                                    in1=factors.unsqueeze(1).to_broadcast([P, 2, count, 2]), op=ALU.mult)
 
         def token_products(s, i):
-            for two in range(2):
-                token_product(s, i, two)
+            for odd in range(2):
+                token_product(s, i, odd, 0, P)
 
         def token_sum(s, engine, batches):
             blk = s % 2
-            views = [parts[(s, two)][:].rearrange("p (b e) -> p b e", b=B)[:, batches, :] for two in range(2)]
+            terms = [products[(s, odd)][:].rearrange("p (b e) -> p b e", b=B)[:, batches, :] for odd in range(2)]
             engine.tensor_tensor(out=result_tile(s)[:, batches, blk * BLOCK:(blk + 1) * BLOCK],
-                                 in0=views[0], in1=views[1], op=ALU.add)
+                                 in0=terms[0], in1=terms[1], op=ALU.add)
 
-        def pair_products(s, two, engine, source):
-            table = tables[(s // UNITS_PER_GROUP, 0, True)]
+        def pair_products(s, odd, engine, u, first, count):
+            batches = slice(first, first + count)
+            factors = pair_tables[s // UNITS_PER_ROUND][:, 1 - odd:3 - odd, :]
             engine.tensor_tensor(
-                out=part_tile(s, two)[:].rearrange("p (c b t) -> p c b t", c=2, b=B),
-                in0=source.rearrange("p (b t) -> p b t", b=B).unsqueeze(1).to_broadcast([P, 2, B, P]),
-                in1=table[:, 1 - two:3 - two, :].unsqueeze(2).to_broadcast([P, 2, B, P]),
-                op=ALU.mult)
+                out=product_tile(s, odd)[:].rearrange("p (c b t) -> p c b t", c=2, b=B)[:, :, batches, :],
+                in0=u.rearrange("p (b t) -> p b t", b=B)[:, batches, :].unsqueeze(1).to_broadcast([P, 2, count, P]),
+                in1=factors.unsqueeze(2).to_broadcast([P, 2, count, P]), op=ALU.mult)
 
-        def odd_products_on_gpsimd(s):
-            odd = small.tile([P, TOKENS], F32, name="odd")
-            nc.scalar.copy(out=odd[:], in_=banks[(s, 1)][:])
-            pair_products(s, 1, nc.gpsimd, odd[:])
+        def gpsimd_products(s):
+            first = B - gpsimd_batches(s)
+            u_odd = small.tile([P, TOKENS], F32, name="u_odd")
+            nc.scalar.copy(out=u_odd[:, first * P:], in_=banks[(s, 1)][:, first * P:])
+            pair_products(s, 1, nc.gpsimd, u_odd[:], first, B - first)
 
-        def pair_sums(s):
-            blk = s % 2
-            views = [parts[(s, two)][:].rearrange("p (c b t) -> p c b t", c=2, b=B) for two in range(2)]
-            for i in range(2):
-                bank = tpsum.tile([P, 4, P], F32, name="tbank")
-                for bb in range(2):
-                    for c in range(2):
-                        for two in range(2):
-                            nc.tensor.matmul(out=bank[:, 2 * bb + c, :], lhsT=views[two][:, c, 2 * i + bb, :],
-                                             rhs=ident[:], is_transpose=True, start=(two == 0), stop=(two == 1))
-                dst = result_tile(s)[:, 2 * i:2 * i + 2, blk * BLOCK:(blk + 1) * BLOCK]
-                nc.scalar.copy(out=dst.rearrange("p b (m c) -> p b m c", c=2),
-                               in_=bank[:].rearrange("p (b c) m -> p b m c", c=2))
+        def pair_sums(s, i):
+            terms = [products[(s, odd)][:].rearrange("p (c b t) -> p c b t", c=2, b=B) for odd in range(2)]
+            bank = tpsum.tile([P, 4, P], F32, name="tbank")
+            for bb in range(2):
+                for c in range(2):
+                    for odd in range(2):
+                        nc.tensor.matmul(out=bank[:, 2 * bb + c, :], lhsT=terms[odd][:, c, 2 * i + bb, :],
+                                         rhs=ident[:], is_transpose=True, start=(odd == 0), stop=(odd == 1))
+            dst = result_tile(s)[:, 2 * i:2 * i + 2, 0:BLOCK]
+            nc.scalar.copy(out=dst.rearrange("p b (m c) -> p b m c", c=2),
+                           in_=bank[:].rearrange("p (b c) m -> p b m c", c=2))
 
-        x0, q0, k0 = ("x", 0), ("w", 0, 0), ("w", 1, 0)
-        whole_turns(0, slice(0, P))
-        extend_freq(P, 4)
-        fraction(0, slice(0, P))
+        x_first, q_first, k_first = ("x", 0), ("w", 0, 0), ("w", 1, 0)
+        first_pairs, other_pairs, all_pairs = slice(0, P), slice(P, PAIRS), slice(0, PAIRS)
+        whole_turns(0, first_pairs)
+        extend_freq(P, PAIRS // P)
+        fraction(0, first_pairs)
         make_token_table(0, [0])
-        whole_turns(0, slice(P, E // 2))
-        whole_turns(1)
-        fraction(0, slice(P, E // 2))
-        fraction(1)
-        transpose_rows(x0, 0)
-        whole_turns(2)
-        quantize_x_tile(x0, 0)
-        fraction(2)
-        transpose_rows(q0, 0)
-        transpose_rows(q0, 1)
-        whole_turns(3)
-        quantize_w_block(q0, 0)
-        transpose_rows(x0, 1)
-        quantize_x_tile(x0, 1)
-        fraction(3)
-        transpose_rows(x0, 2)
+        whole_turns(0, other_pairs)
+        whole_turns(1, all_pairs)
+        fraction(0, other_pairs)
+        fraction(1, all_pairs)
+        transpose_slot(x_first, 0)
+        whole_turns(2, all_pairs)
+        quantize_x_slot(x_first, 0)
+        fraction(2, all_pairs)
+        transpose_slot(q_first, 0)
+        transpose_slot(q_first, 1)
+        whole_turns(3, all_pairs)
+        quantize_w_block(q_first, 0)
+        transpose_slot(x_first, 1)
+        quantize_x_slot(x_first, 1)
+        fraction(3, all_pairs)
+        transpose_slot(x_first, 2)
         multiply_bank(0, 0)
         make_token_table(0, [1])
-        quantize_x_tile(x0, 2)
-        transpose_rows(x0, 3)
-        transpose_rows(q0, 2)
-        transpose_rows(q0, 3)
+        quantize_x_slot(x_first, 2)
+        transpose_slot(x_first, 3)
+        transpose_slot(q_first, 2)
+        transpose_slot(q_first, 3)
         token_products(0, 0)
-        quantize_x_tile(x0, 3)
+        quantize_x_slot(x_first, 3)
         multiply_bank(0, 1)
-        transpose_rows(k0, 0)
-        transpose_rows(k0, 1)
+        transpose_slot(k_first, 0)
+        transpose_slot(k_first, 1)
+        quantize_w_block(q_first, 1)
 
-        to_transpose = {0: [(k0, 2), (k0, 3)], 1: [(("x", 1), b) for b in range(B)]}
-        queue = [(key, slot) for key in (("x", 2), ("w", 0, 1), ("x", 3), ("w", 1, 1)) for slot in range(4)]
-        s = 2
-        while queue:
-            count = 1 if pairs_on_partitions(s - 1) else 2
-            to_transpose[s], queue = queue[:count], queue[count:]
-            s += 1
-        quantize_w_block(q0, 1)
-        inside_unit = {0: lambda: quantize_w_block(k0, 0), 1: lambda: quantize_w_block(k0, 1),
-                       2: lambda: quantize_all(("x", 1))}
-        to_quantize = {7: [("x", 2)], 11: [("x", 3), ("w", 0, 1)], 15: [("w", 1, 1)]}
+        to_transpose = {0: [(k_first, 2), (k_first, 3)], 1: [(("x", 1), b) for b in range(SLOTS)]}
+        later = [(key, slot) for key in (("x", 2), ("w", 0, 1), ("x", 3), ("w", 1, 1)) for slot in range(SLOTS)]
+        for i in range(0, len(later), SLOTS_PER_STEP):
+            to_transpose[2 + i // SLOTS_PER_STEP] = later[i:i + SLOTS_PER_STEP]
+
+        def quantize_in_step(s):
+            if s < 2:
+                quantize_w_block(k_first, s)
+            elif s == 2:
+                quantize_operand(("x", 1))
+            else:
+                for key in QUANTIZE_AFTER:
+                    if QUANTIZE_AFTER[key] == s:
+                        quantize_operand(key)
 
         for s in range(UNITS):
-            group, place = divmod(s, UNITS_PER_GROUP)
-            last = s == UNITS - 1
-            for key in to_quantize.get(s, []):
-                quantize_all(key)
-            if not last:
+            rnd, place = divmod(s, UNITS_PER_ROUND)
+            quantizes = s <= 2 or s in QUANTIZE_AFTER.values()
+            unit_stores = rnd >= ROUNDS - 2
+            bank_stores = rnd == ROUNDS - 1
+
+            if s + 1 < UNITS:
                 multiply_bank(s + 1, 0)
                 multiply_bank(s + 1, 1)
-                if gpsimd_multiplies(s + 1):
-                    odd_products_on_gpsimd(s + 1)
-            if s > 0 and pairs_on_partitions(s - 1):
-                pair_sums(s - 1)
-                if last:
-                    store(s - 1, slice(0, B), [0])
+                if gpsimd_batches(s + 1):
+                    gpsimd_products(s + 1)
+            if is_pair_unit(s - 1):
+                for i in range(2):
+                    pair_sums(s - 1, i)
+                    if bank_stores:
+                        store(s - 1, slice(2 * i, 2 * i + 2), [0])
             for key, slot in to_transpose.get(s, []):
-                transpose_rows(key, slot)
-            if group + 1 < HALVES * GROUPS:
-                if place == 1:
-                    make_pair_table(group + 1)
+                transpose_slot(key, slot)
+            if is_pair_unit(s - 1) and unit_stores and not bank_stores:
+                store(s - 1, slice(0, B), [0])
+
+            if rnd + 1 < ROUNDS:
+                coming = range((rnd + 1) * UNITS_PER_ROUND, (rnd + 2) * UNITS_PER_ROUND)
+                if place == 1 and any(is_pair_unit(n) for n in coming):
+                    make_pair_table(rnd + 1)
                 if place == 2:
-                    make_token_table(group + 1, token_blocks(group + 1))
-            if pairs_on_partitions(s):
-                pair_products(s, 0, nc.vector, banks[(s, 0)][:])
-                if not gpsimd_multiplies(s):
-                    pair_products(s, 1, nc.vector, banks[(s, 1)][:])
-            elif last:
+                    make_token_table(rnd + 1, sorted({n % 2 for n in coming if not is_pair_unit(n)}))
+
+            if is_pair_unit(s):
+                pair_products(s, 0, nc.vector, banks[(s, 0)][:], 0, B)
+                pair_products(s, 1, nc.vector, banks[(s, 1)][:], 0, B - gpsimd_batches(s))
+                if quantizes:
+                    quantize_in_step(s)
+            elif s == UNITS - 1:
                 for i, engine in enumerate((nc.gpsimd, nc.vector)):
                     token_products(s, i)
                     token_sum(s, engine, slice(2 * i, 2 * i + 2))
@@ -384,13 +393,15 @@ def tile_attention_pa_kernel(tc, x, wq, wk, out_0, out_1):
             else:
                 if s > 0:
                     token_products(s, 0)
-                if s in inside_unit:
-                    token_product(s, 1, 0)
+                if quantizes:
+                    token_product(s, 1, 0, 0, P)
                     token_product(s, 1, 1, 0, P - HELD_BACK)
-                    inside_unit[s]()
+                    quantize_in_step(s)
                     token_product(s, 1, 1, P - HELD_BACK, HELD_BACK)
                 else:
                     token_products(s, 1)
                 token_sum(s, nc.gpsimd, slice(0, B))
-                if s % 2 == 1:
+                if unit_stores:
+                    store(s, slice(0, B), [1])
+                elif s % 2 == 1:
                     store(s, slice(0, B), [0, 1])

import math
from contextlib import ExitStack

import concourse.mybir as mybir
from concourse.masks import make_identity

B, S, D, E = 4, 512, 1024, 1024
THETA = 10000.0
FLOPS = 2 * 2 * B * S * D * E

F32 = mybir.dt.float32
BF16 = mybir.dt.bfloat16
I32 = mybir.dt.int32
U32 = mybir.dt.uint32
U8 = mybir.dt.uint8
E5M2X4 = mybir.dt.float8_e5m2_x4
E4M3X4 = mybir.dt.float8_e4m3fn_x4
ALU = mybir.AluOpType
ACT = mybir.ActivationFunctionType

P = 128
PACK = 4
PASSES = D // (P * PACK)
PASS_PAIRS = P * PACK // 2
PAIRS = E // 2
TOKENS = B * P
BLOCK = 2 * P
POSITION_GROUPS = S // P
SLOTS = 4
UNITS_PER_ROUND = 4
ROUNDS = 2 * POSITION_GROUPS
UNITS = ROUNDS * UNITS_PER_ROUND

FIRST_PAIR_UNIT = 10
GPSIMD_SHARE = 3
SLOTS_PER_STEP = 2
HELD_BACK = 16
QUANTIZE_AFTER = {("x", 2): 6, ("x", 3): 10, ("w", 0, 1): 10, ("w", 1, 1): 14}


def unit_indices(s):
    half, group = divmod(s // UNITS_PER_ROUND, POSITION_GROUPS)
    proj, blk = divmod(s % UNITS_PER_ROUND, 2)
    return half, group, proj, blk


def is_pair_unit(s):
    return s >= FIRST_PAIR_UNIT and s % 2 == 0


def gpsimd_batches(s):
    if not is_pair_unit(s) or s in QUANTIZE_AFTER.values() or s == UNITS - 2:
        return 0
    return GPSIMD_SHARE


def tile_attention_pa_kernel(tc, x, wq, wk, out_0, out_1):
    nc = tc.nc
    weights = (wq, wk)
    outs = (out_0, out_1)

    with ExitStack() as ctx:
        keep = ctx.enter_context(tc.tile_pool(name="keep", bufs=1))
        stage = ctx.enter_context(tc.tile_pool(name="stage", bufs=3))
        small = ctx.enter_context(tc.tile_pool(name="small", bufs=2))
        tabs = ctx.enter_context(tc.tile_pool(name="tabs", bufs=3))
        work = ctx.enter_context(tc.tile_pool(name="work", bufs=4))
        res = ctx.enter_context(tc.tile_pool(name="res", bufs=3))
        tpsum = ctx.enter_context(tc.psum_pool(name="tpsum", bufs=3))
        mpsum = ctx.enter_context(tc.psum_pool(name="mpsum", bufs=5))
        ctx.enter_context(tc.manual_schedule())

        raw = {}

        def load_x_slot(group, b):
            rows = keep.tile([P, D], BF16, name=f"x_raw_{group}_{b}")
            nc.sync.dma_start(out=rows[:], in_=x[b, group * P:(group + 1) * P, :])
            raw[(("x", group), b)] = rows[:]

        def load_x_group(group):
            rows = keep.tile([P, B, D], BF16, name=f"x_raw_{group}")
            nc.sync.dma_start(out=rows[:], in_=x[:, group * P:(group + 1) * P, :].rearrange("b p k -> p b k"))
            for b in range(B):
                raw[(("x", group), b)] = rows[:, b, :]

        def load_w_block(proj, half, blk):
            rows = keep.tile([P, 2, D], BF16, name=f"w_raw_{proj}_{half}_{blk}")
            first = (2 * half + blk) * BLOCK
            src = weights[proj][first:first + BLOCK, :].rearrange("(m odd) k -> m odd k", odd=2)
            nc.sync.dma_start(out=rows[:], in_=src)
            for odd in range(2):
                raw[(("w", proj, half), 2 * blk + odd)] = rows[:, odd, :]

        load_x_slot(0, 0)
        load_w_block(0, 0, 0)
        for b in range(1, B):
            load_x_slot(0, b)
        load_w_block(0, 0, 1)
        load_w_block(1, 0, 0)
        load_w_block(1, 0, 1)
        load_x_group(1)
        load_x_group(2)
        load_w_block(0, 1, 0)
        load_w_block(0, 1, 1)
        load_x_group(3)
        load_w_block(1, 1, 0)
        load_w_block(1, 1, 1)

        position = keep.tile([P, POSITION_GROUPS], F32)
        nc.gpsimd.iota(position[:], pattern=[[P, POSITION_GROUPS]], base=0, channel_multiplier=1,
                       allow_small_or_imprecise_dtypes=True)
        ident = keep.tile([P, P], F32)
        make_identity(nc, ident[:])

        one = keep.tile([P, 1], F32)
        nc.vector.memset(one[:], 1.0)
        freq = keep.tile([P, PAIRS], F32)
        half_pi = keep.tile([P, 1], F32)

        def extend_freq(known, factor):
            for c in range(1, factor):
                nc.vector.tensor_scalar(out=freq[:, c * known:(c + 1) * known], in0=freq[:, 0:known],
                                        scalar1=THETA ** (-2.0 * c * known / E), scalar2=None, op0=ALU.mult)

        for c in range(4):
            nc.vector.tensor_scalar(out=freq[:, c:c + 1], in0=one[:], scalar1=THETA ** (-2.0 * c / E) / (2.0 * math.pi),
                                    scalar2=None, op0=ALU.mult)
        nc.vector.tensor_scalar(out=half_pi[:], in0=one[:], scalar1=math.pi / 2.0, scalar2=None, op0=ALU.mult)
        extend_freq(4, 4)
        extend_freq(16, 4)
        extend_freq(64, 2)

        whole = {}
        frac = keep.tile([P, POSITION_GROUPS, PAIRS], F32)

        def whole_turns(group, pairs):
            if group not in whole:
                whole[group] = small.tile([P, PAIRS], I32, name="whole")
            nc.vector.tensor_scalar(out=whole[group][:, pairs], in0=freq[:, pairs],
                                    scalar1=position[:, group:group + 1], scalar2=None, op0=ALU.mult)

        def fraction(group, pairs):
            nc.vector.scalar_tensor_tensor(out=frac[:, group, pairs], in0=freq[:, pairs],
                                           scalar=position[:, group:group + 1], in1=whole[group][:, pairs],
                                           op0=ALU.mult, op1=ALU.subtract)

        token_tables = {}
        pair_tables = {}

        def fill_table(table, turns, width):
            size = small.tile([P, BLOCK], F32, name="size")
            nc.scalar.activation(out=size[:, :width], in_=turns, func=ACT.Abs)
            nc.scalar.activation(out=table[:, 0, :], in_=turns, func=ACT.Sin, scale=-2.0 * math.pi)
            nc.scalar.activation(out=table[:, 2, :], in_=turns, func=ACT.Sin, scale=2.0 * math.pi)
            nc.scalar.activation(out=table[:, 1, :], in_=size[:, :width], func=ACT.Sin, scale=-2.0 * math.pi,
                                 bias=half_pi[:])

        def make_token_table(rnd, blocks):
            half, group = divmod(rnd, POSITION_GROUPS)
            width = len(blocks) * P
            table = tabs.tile([P, 3, width], F32, name="token_table")
            first = (2 * half + blocks[0]) * P
            fill_table(table[:], frac[:, group, first:first + width], width)
            for i, blk in enumerate(blocks):
                token_tables[(rnd, blk)] = table[:, :, i * P:(i + 1) * P]

        def make_pair_table(rnd):
            half, group = divmod(rnd, POSITION_GROUPS)
            bank = tpsum.tile([P, 4, P], F32, name="tbank")
            nc.tensor.transpose(bank[:, 0, :], frac[:, group, 2 * half * P:(2 * half + 1) * P], ident[:])
            table = tabs.tile([P, 3, P], F32, name="pair_table")
            fill_table(table[:], bank[:, 0, :], P)
            pair_tables[rnd] = table[:]

        staged = {}
        codes = {}
        scales = {}

        def transpose_slot(key, slot):
            runs = 1 if key[0] == "x" else 2
            width = SLOTS * P // runs
            if slot == 0:
                staged[key] = stage.tile([P, runs, PASSES, width * PACK], BF16, name="staged", align_bytes=256)
                suffix = "_".join(str(v) for v in key)
                codes[key] = keep.tile([P, runs, PASSES, width], U32, name="codes_" + suffix, align_bytes=256)
                scales[key] = keep.tile([P, runs, PASSES, width], U8, name="scales_" + suffix, align_bytes=256)
            k_pairs = raw[(key, slot)].bitcast(F32)
            bank = tpsum.tile([P, 4, P], F32, name="tbank")
            for g in range(PASSES):
                for u in range(2):
                    nc.tensor.transpose(bank[:, 2 * g + u, :], k_pairs[:, g * PASS_PAIRS + u:(g + 1) * PASS_PAIRS:2],
                                        ident[:])
            run, first = divmod(slot * P, width)
            dst = staged[key][:, run, :, PACK * first:PACK * (first + P)].bitcast(F32)
            nc.scalar.copy(out=dst.rearrange("p g (c u) -> p g c u", u=2),
                           in_=bank[:].rearrange("p (g u) c -> p g c u", u=2))

        def quantize_operand(key):
            fmt = E5M2X4 if key[0] == "x" else E4M3X4
            nc.vector.quantize_mx(out=codes[key][:].rearrange("p r g c -> p (r g c)").bitcast(fmt),
                                  scales=scales[key][:].rearrange("p r g c -> p (r g c)"),
                                  in_=staged[key][:].rearrange("p r g c -> p (r g c)"))

        def quantize_w_block(key, blk):
            nc.vector.quantize_mx(out=codes[key][:, blk].rearrange("p g c -> p (g c)").bitcast(E4M3X4),
                                  scales=scales[key][:, blk].rearrange("p g c -> p (g c)"),
                                  in_=staged[key][:, blk].rearrange("p g c -> p (g c)"))

        def quantize_x_slot(key, b):
            for g in range(PASSES):
                nc.vector.quantize_mx(out=codes[key][:, 0, g, b * P:(b + 1) * P].bitcast(E5M2X4),
                                      scales=scales[key][:, 0, g, b * P:(b + 1) * P],
                                      in_=staged[key][:, 0, g, PACK * b * P:PACK * (b + 1) * P])

        banks = {}

        def multiply_bank(s, i):
            half, group, proj, blk = unit_indices(s)
            x_codes, x_scales = codes[("x", group)], scales[("x", group)]
            w_codes, w_scales = codes[("w", proj, half)], scales[("w", proj, half)]
            bank = mpsum.tile([P, TOKENS], F32, name="mbank")
            banks[(s, i)] = bank
            if is_pair_unit(s):
                cols = slice(i * P, (i + 1) * P)
                for g in range(PASSES):
                    nc.tensor.matmul_mx(out=bank[:], lhsT=w_codes[:, blk, g, cols].bitcast(E4M3X4),
                                        lhsT_scale=w_scales[:, blk, g, cols],
                                        rhs=x_codes[:, 0, g, :].bitcast(E5M2X4), rhs_scale=x_scales[:, 0, g, :],
                                        start=(g == 0), stop=(g == PASSES - 1))
            else:
                for bb in range(2):
                    cols = slice((2 * i + bb) * P, (2 * i + bb + 1) * P)
                    for g in range(PASSES):
                        nc.tensor.matmul_mx(out=bank[:, bb * BLOCK:(bb + 1) * BLOCK],
                                            lhsT=x_codes[:, 0, g, cols].bitcast(E5M2X4),
                                            lhsT_scale=x_scales[:, 0, g, cols],
                                            rhs=w_codes[:, blk, g, :].bitcast(E4M3X4),
                                            rhs_scale=w_scales[:, blk, g, :],
                                            start=(g == 0), stop=(g == PASSES - 1))

        products = {}
        results = {}

        def product_tile(s, odd):
            if (s, odd) not in products:
                products[(s, odd)] = work.tile([P, 2 * TOKENS], F32, name=f"products_{odd}")
            return products[(s, odd)]

        def result_tile(s):
            if s // 2 not in results:
                results[s // 2] = res.tile([P, B, 2 * BLOCK], F32, name="result")
            return results[s // 2]

        def store(s, batches, blocks):
            half, group, proj, blk = unit_indices(s)
            cols = slice(blocks[0] * BLOCK, (blocks[-1] + 1) * BLOCK)
            dst = outs[proj][batches, group * P:(group + 1) * P, half * 2 * BLOCK:(half + 1) * 2 * BLOCK]
            nc.sync.dma_start(out=dst[:, :, cols].rearrange("b p e -> p b e"), in_=results[s // 2][:, batches, cols])

        def token_product(s, i, odd, first, count):
            u = banks[(s, i)][:].rearrange("p (b odd m) -> p b odd m", odd=2, m=P)
            pairs = slice(first, first + count)
            dst = product_tile(s, odd)[:, i * TOKENS:(i + 1) * TOKENS]
            factors = token_tables[(s // UNITS_PER_ROUND, s % 2)][:, 1 - odd:3 - odd, pairs].rearrange("p c m -> p m c")
            nc.vector.tensor_tensor(out=dst.rearrange("p (b m c) -> p b m c", m=P, c=2)[:, :, pairs, :],
                                    in0=u[:, :, odd, pairs].unsqueeze(3).to_broadcast([P, 2, count, 2]),
                                    in1=factors.unsqueeze(1).to_broadcast([P, 2, count, 2]), op=ALU.mult)

        def token_products(s, i):
            for odd in range(2):
                token_product(s, i, odd, 0, P)

        def token_sum(s, engine, batches):
            blk = s % 2
            terms = [products[(s, odd)][:].rearrange("p (b e) -> p b e", b=B)[:, batches, :] for odd in range(2)]
            engine.tensor_tensor(out=result_tile(s)[:, batches, blk * BLOCK:(blk + 1) * BLOCK],
                                 in0=terms[0], in1=terms[1], op=ALU.add)

        def pair_products(s, odd, engine, u, first, count):
            batches = slice(first, first + count)
            factors = pair_tables[s // UNITS_PER_ROUND][:, 1 - odd:3 - odd, :]
            engine.tensor_tensor(
                out=product_tile(s, odd)[:].rearrange("p (c b t) -> p c b t", c=2, b=B)[:, :, batches, :],
                in0=u.rearrange("p (b t) -> p b t", b=B)[:, batches, :].unsqueeze(1).to_broadcast([P, 2, count, P]),
                in1=factors.unsqueeze(2).to_broadcast([P, 2, count, P]), op=ALU.mult)

        def gpsimd_products(s):
            first = B - gpsimd_batches(s)
            u_odd = small.tile([P, TOKENS], F32, name="u_odd")
            nc.scalar.copy(out=u_odd[:, first * P:], in_=banks[(s, 1)][:, first * P:])
            pair_products(s, 1, nc.gpsimd, u_odd[:], first, B - first)

        def pair_sums(s, i):
            terms = [products[(s, odd)][:].rearrange("p (c b t) -> p c b t", c=2, b=B) for odd in range(2)]
            bank = tpsum.tile([P, 4, P], F32, name="tbank")
            for bb in range(2):
                for c in range(2):
                    for odd in range(2):
                        nc.tensor.matmul(out=bank[:, 2 * bb + c, :], lhsT=terms[odd][:, c, 2 * i + bb, :],
                                         rhs=ident[:], is_transpose=True, start=(odd == 0), stop=(odd == 1))
            dst = result_tile(s)[:, 2 * i:2 * i + 2, 0:BLOCK]
            nc.scalar.copy(out=dst.rearrange("p b (m c) -> p b m c", c=2),
                           in_=bank[:].rearrange("p (b c) m -> p b m c", c=2))

        x_first, q_first, k_first = ("x", 0), ("w", 0, 0), ("w", 1, 0)
        first_pairs, other_pairs, all_pairs = slice(0, P), slice(P, PAIRS), slice(0, PAIRS)
        whole_turns(0, first_pairs)
        extend_freq(P, PAIRS // P)
        fraction(0, first_pairs)
        make_token_table(0, [0])
        whole_turns(0, other_pairs)
        whole_turns(1, all_pairs)
        fraction(0, other_pairs)
        fraction(1, all_pairs)
        transpose_slot(x_first, 0)
        whole_turns(2, all_pairs)
        quantize_x_slot(x_first, 0)
        fraction(2, all_pairs)
        transpose_slot(q_first, 0)
        transpose_slot(q_first, 1)
        whole_turns(3, all_pairs)
        quantize_w_block(q_first, 0)
        transpose_slot(x_first, 1)
        quantize_x_slot(x_first, 1)
        fraction(3, all_pairs)
        transpose_slot(x_first, 2)
        multiply_bank(0, 0)
        make_token_table(0, [1])
        quantize_x_slot(x_first, 2)
        transpose_slot(x_first, 3)
        transpose_slot(q_first, 2)
        transpose_slot(q_first, 3)
        token_products(0, 0)
        quantize_x_slot(x_first, 3)
        multiply_bank(0, 1)
        transpose_slot(k_first, 0)
        transpose_slot(k_first, 1)
        quantize_w_block(q_first, 1)

        to_transpose = {0: [(k_first, 2), (k_first, 3)], 1: [(("x", 1), b) for b in range(SLOTS)]}
        later = [(key, slot) for key in (("x", 2), ("w", 0, 1), ("x", 3), ("w", 1, 1)) for slot in range(SLOTS)]
        for i in range(0, len(later), SLOTS_PER_STEP):
            to_transpose[2 + i // SLOTS_PER_STEP] = later[i:i + SLOTS_PER_STEP]

        def quantize_in_step(s):
            if s < 2:
                quantize_w_block(k_first, s)
            elif s == 2:
                quantize_operand(("x", 1))
            else:
                for key in QUANTIZE_AFTER:
                    if QUANTIZE_AFTER[key] == s:
                        quantize_operand(key)

        for s in range(UNITS):
            rnd, place = divmod(s, UNITS_PER_ROUND)
            quantizes = s <= 2 or s in QUANTIZE_AFTER.values()
            unit_stores = rnd >= ROUNDS - 2
            bank_stores = rnd == ROUNDS - 1

            if s + 1 < UNITS:
                multiply_bank(s + 1, 0)
                multiply_bank(s + 1, 1)
                if gpsimd_batches(s + 1):
                    gpsimd_products(s + 1)
            if is_pair_unit(s - 1):
                for i in range(2):
                    pair_sums(s - 1, i)
                    if bank_stores:
                        store(s - 1, slice(2 * i, 2 * i + 2), [0])
            for key, slot in to_transpose.get(s, []):
                transpose_slot(key, slot)
            if is_pair_unit(s - 1) and unit_stores and not bank_stores:
                store(s - 1, slice(0, B), [0])

            if rnd + 1 < ROUNDS:
                coming = range((rnd + 1) * UNITS_PER_ROUND, (rnd + 2) * UNITS_PER_ROUND)
                if place == 1 and any(is_pair_unit(n) for n in coming):
                    make_pair_table(rnd + 1)
                if place == 2:
                    make_token_table(rnd + 1, sorted({n % 2 for n in coming if not is_pair_unit(n)}))

            if is_pair_unit(s):
                pair_products(s, 0, nc.vector, banks[(s, 0)][:], 0, B)
                pair_products(s, 1, nc.vector, banks[(s, 1)][:], 0, B - gpsimd_batches(s))
                if quantizes:
                    quantize_in_step(s)
            elif s == UNITS - 1:
                for i, engine in enumerate((nc.gpsimd, nc.vector)):
                    token_products(s, i)
                    token_sum(s, engine, slice(2 * i, 2 * i + 2))
                    store(s, slice(2 * i, 2 * i + 2), [1])
            else:
                if s > 0:
                    token_products(s, 0)
                if quantizes:
                    token_product(s, 1, 0, 0, P)
                    token_product(s, 1, 1, 0, P - HELD_BACK)
                    quantize_in_step(s)
                    token_product(s, 1, 1, P - HELD_BACK, HELD_BACK)
                else:
                    token_products(s, 1)
                token_sum(s, nc.gpsimd, slice(0, B))
                if unit_stores:
                    store(s, slice(0, B), [1])
                elif s % 2 == 1:
                    store(s, slice(0, B), [0, 1])
